import numpy as np
import ml_dtypes


def mxq(x, axis, fmt="e4m3"):
    dtype, down = {"e4m3": (ml_dtypes.float8_e4m3fn, 7), "e5m2": (ml_dtypes.float8_e5m2, 14)}[fmt]
    v = np.moveaxis(np.asarray(x, np.float32).astype(ml_dtypes.bfloat16).astype(np.float64), axis, -1)
    blocks = v.reshape(v.shape[:-1] + (-1, 32))
    amax = np.abs(blocks).max(-1, keepdims=True)
    byte = np.maximum(np.where(amax > 0, np.frexp(amax)[1] - 1 + 127, 0) - down, 1)
    scale = np.exp2(byte - 127.0)
    codes = (blocks / scale).astype(np.float32).astype(dtype).astype(np.float64)
    return np.moveaxis((codes * scale).reshape(v.shape), -1, axis)


WIDE = False


def mx_kscale(k):
    if not WIDE:
        return np.ones(k)
    levels = np.array([18, -18])
    if k % 512:
        return np.exp2(np.random.permutation(np.resize(levels, k // 32))).repeat(32)
    a = np.empty((k // 512, 16))
    for p in range(k // 512):
        a[p, :8] = np.random.permutation(np.resize(levels, 8))
        for g in range(8):
            far = levels[np.abs(levels - a[p, g]) >= 10]
            a[p, g + 8] = far[np.random.randint(len(far))]
    return np.exp2(a.ravel()).repeat(32)


BF16 = ml_dtypes.bfloat16


def bf(x):
    return np.asarray(x, np.float32).astype(BF16)


def f64(x):
    return np.asarray(x).astype(np.float64)


M, N, IN_CH, HID, DEG = 2560, 2560, 512, 512, 24


def setup_inputs():
    u = mx_kscale(M)
    v = mx_kscale(HID)
    s = mx_kscale(N)
    x0 = bf(np.random.standard_normal((N, IN_CH)))
    adj0 = bf(np.random.uniform(size=(M, N)) < DEG / N)
    w0 = bf(np.random.standard_normal((IN_CH, HID)) * 2.0 / np.sqrt(IN_CH))
    b_in = bf(np.random.standard_normal(HID) * 0.3)
    g = bf(np.random.standard_normal((M, HID)) * np.exp2(np.random.randint(-6, 1, (M, 1))) * 4.0 * u[:, None] * v)
    deg = np.sum(f64(adj0), axis=1)
    return {"x": bf(f64(x0) * s[:, None]),
            "adj": bf(f64(adj0) / u[:, None] / s[None, :]),
            "W_in": bf(f64(w0) / v),
            "b_in": b_in,
            "deg": np.asarray(deg, np.float32),
            "grad_out": g}


def reference(x, adj, W_in, b_in, deg, grad_out):
    dz2 = f64(grad_out) / (f64(deg)[:, None] + 1.0)
    dh = mxq(f64(adj), 0, "e4m3").T @ mxq(dz2, 0, "e5m2")
    dz1 = dh
    dx = mxq(dz1, 1, "e5m2") @ mxq(f64(W_in), 1, "e4m3").T
    dW = mxq(f64(x), 0, "e4m3").T @ mxq(dz1, 0, "e5m2")
    return dx, dW

@@ -1,0 +1,274 @@
+from contextlib import ExitStack
+
+import concourse.mybir as mybir
+from concourse.masks import make_identity
+
+N = 2560
+IN = 512
+HID = 512
+FLOPS = 2 * (N * N * HID + 2 * N * IN * HID)
+BYTES = 2 * (N * IN + N * N + IN * HID + N * HID) + 4 * (N + N * IN + IN * HID)
+
+F32 = mybir.dt.float32
+BF16 = mybir.dt.bfloat16
+U32 = mybir.dt.uint32
+U8 = mybir.dt.uint8
+E4 = mybir.dt.float8_e4m3fn_x4
+E5 = mybir.dt.float8_e5m2_x4
+MULT = mybir.AluOpType.mult
+
+P = 128
+B = 512
+NB = N // B
+
+
+def tile_allgnn_pa_v_kernel(tc, x, adj, W_in, b_in, deg, grad_out, out_0, out_1):
+    nc = tc.nc
+    with ExitStack() as ctx:
+        sb = ctx.enter_context(tc.tile_pool(name="sb", bufs=1))
+        ps = ctx.enter_context(tc.psum_pool(name="ps", bufs=1))
+        ctx.enter_context(tc.manual_schedule())
+
+        def new(shape, dt, tag, bufs):
+            return sb.tile(shape, dt, tag=tag, name=tag, bufs=bufs, align_bytes=64)
+
+        def bank(tag):
+            return ps.tile([P, B], F32, tag=tag, name=tag, bufs=1)
+
+        def codes(tag, bufs):
+            return new([P, B], U32, tag + "c", bufs), new([P, B], U8, tag + "s", bufs)
+
+        def quantize(src, tag, bufs, fmt):
+            c, s = codes(tag, bufs)
+            nc.vector.quantize_mx(out=c[:].bitcast(fmt), scales=s[:], in_=src[:])
+            return c, s
+
+        def mm(out, l, lcols, lfmt, r, rfmt, start, stop):
+            nc.tensor.matmul_mx(
+                out=out[:],
+                lhsT=l[0][:, lcols].bitcast(lfmt),
+                lhsT_scale=l[1][:, lcols],
+                rhs=r[0][:].bitcast(rfmt),
+                rhs_scale=r[1][:],
+                start=start,
+                stop=stop,
+            )
+
+        def rows(ap, g, cols):
+            return ap[B * g : B * (g + 1), cols].rearrange("(p j) w -> p j w", j=4)
+
+        def copy(eng, out, in_):
+            if eng == "S":
+                nc.scalar.copy(out=out, in_=in_)
+            else:
+                nc.vector.tensor_copy(out=out, in_=in_)
+
+        def interleave(eng, src):
+            dst = new([P, 4 * B], BF16, "ilv", 7)
+            copy(
+                eng,
+                dst[:].rearrange("p (w i j) -> p w j i", i=4, j=4),
+                src.rearrange("p j (w i) -> p w j i", i=4),
+            )
+            return dst
+
+        full = slice(0, B)
+
+        r = new([P, NB, 4], F32, "deg", 1)
+        nc.sync.dma_start(out=r[:], in_=deg.rearrange("(g p j) -> p g j", p=P, j=4))
+        ident = new([P, P], F32, "ident", 1)
+        make_identity(nc, ident[:])
+
+        def load512(ap, g):
+            t = new([P, 4, B], BF16, "raw512", 11)
+            nc.sync.dma_start(out=t[:], in_=rows(ap, g, full))
+            return t
+
+        graw, araw = [], {}
+        w_raw = new([P, 4, HID], BF16, "wraw", 1)
+        for g in range(NB):
+            if g == NB - 1:
+                nc.sync.dma_start(out=w_raw[:], in_=W_in.rearrange("(a p) h -> p a h", p=P))
+            graw.append(load512(grad_out, g))
+            araw[0, g] = load512(adj, g)[:]
+
+        def load_pair(c, g):
+            t = new([P, 4, 2 * B], BF16, "raw1024", 8)
+            nc.sync.dma_start(out=t[:], in_=rows(adj, g, slice(B * c, B * (c + 2))))
+            araw[c, g] = t[:, :, 0:B]
+            araw[c + 1, g] = t[:, :, B : 2 * B]
+
+        for g in range(NB):
+            load_pair(1, g)
+
+        nc.vector.tensor_scalar_add(r[:], r[:], 1.0)
+        rec = new([P, NB, 4], F32, "rec", 1)
+        nc.vector.reciprocal(out=rec[:], in_=r[:])
+
+        def scale_g(g):
+            t = new([P, 4, HID], BF16, "g2", 2)
+            for j in range(4):
+                nc.vector.tensor_scalar_mul(t[:, j, :], graw[g][:, j, :], rec[:, g, j : j + 1])
+            return t
+
+        def interleave_g(src):
+            dst = new([P, 4 * HID], BF16, "ilv", 7)
+            nc.vector.tensor_copy(
+                out=dst[:].rearrange("p (t m j) -> p t m j", t=4, j=4),
+                in_=src[:].rearrange("p j (m t) -> p t m j", t=4),
+            )
+            return dst
+
+        dh = {}
+        gcodes, xcodes, kcodes = [], [], []
+        ailv = {}
+
+        def inter(eng, c, g):
+            ailv[c, g] = interleave(eng, araw[c, g])
+
+        def quant_mul(c, g):
+            a = quantize(ailv[c, g], "a", 4, E4)
+            for t in range(4):
+                if g == 0:
+                    dh[t] = bank("dh" + str(t))
+                mm(dh[t], gcodes[g], slice(P * t, P * (t + 1)), E5, a, E4, g == 0, g == NB - 1)
+
+        w_words = w_raw[:].bitcast(F32)
+        w_ilv = []
+        wc = []
+
+        def w_transpose():
+            dst = new([P, 4 * IN], BF16, "ilv", 7)
+            dv = dst[:].bitcast(F32).rearrange("p (b a i u) -> p b a i u", b=2, a=2, u=2)
+            for b in range(2):
+                xt = bank("w" + str(b))[:].rearrange("p (a u i) -> p a u i", a=2, u=2)
+                for a in range(2):
+                    for u in range(2):
+                        nc.tensor.transpose(xt[:, a, u, :], w_words[:, 2 * b + a, u : HID // 2 : 2], ident[:])
+                nc.scalar.copy(out=dv[:, b], in_=xt.rearrange("p a u i -> p a i u"))
+            w_ilv.append(dst)
+
+        g2 = scale_g(0)
+        inter("S", 0, 0)
+        gi = interleave_g(g2)
+        for g in range(1, NB):
+            g2 = scale_g(g)
+            inter("S", 0, g)
+            gcodes.append(quantize(gi, "g", NB, E5))
+            gi = interleave_g(g2)
+            quant_mul(0, g - 1)
+        x_raw = [load512(x, 0), load512(x, 1)]
+        for g in range(3):
+            load_pair(3, g)
+        for g in range(2, NB):
+            x_raw.append(load512(x, g))
+        gcodes.append(quantize(gi, "g", NB, E5))
+        w_transpose()
+        inter("S", 1, 0)
+        quant_mul(0, NB - 1)
+
+        def evict(engs):
+            d = new([P, 4, B], BF16, "d", 2)
+            for t in range(4):
+                copy(engs[t], d[:, t, :], dh[t][:])
+            return d
+
+        def flip(d, tags):
+            words = d[:].bitcast(F32)
+            out = []
+            for b in range(2):
+                xt = bank(tags[b])[:].rearrange("p (t u m) -> p t u m", t=2, u=2)
+                for t in range(2):
+                    for u in range(2):
+                        nc.tensor.transpose(xt[:, t, u, :], words[:, 2 * b + t, u : B // 2 : 2], ident[:])
+                out.append(xt)
+            return out
+
+        def flip_copy(xts, eng):
+            dst = new([P, 4 * HID], BF16, "ilv", 7)
+            dv = dst[:].bitcast(F32).rearrange("p (b t m u) -> p b t m u", b=2, t=2, u=2)
+            for b in range(2):
+                copy(eng, dv[:, b], xts[b].rearrange("p t u m -> p t m u"))
+            return dst
+
+        def dx_mul(h, tags):
+            out = []
+            for b in range(4):
+                o = bank(tags[b])
+                mm(o, h, slice(P * b, P * (b + 1)), E5, wc[0], E4, True, True)
+                out.append(o)
+            return out
+
+        def dx_store(c, b, o, eng):
+            t = new([P, IN], F32, "out", 6)
+            copy(eng, t[:], o[:])
+            n0 = B * c + P * b
+            nc.sync.dma_start(out=out_0[n0 : n0 + P, :], in_=t[:])
+
+        acc = {}
+
+        def dw_mul(a, cs):
+            for c in cs:
+                if c == 0:
+                    acc[a] = bank("w" + str((a + 2) % 4))
+                mm(acc[a], xcodes[c], slice(P * a, P * (a + 1)), E4, kcodes[c], E5, c == 0, c == NB - 1)
+
+        def quant_x(src):
+            xcodes.append(quantize(src, "x", NB, E4))
+
+        for c in range(1, NB):
+            d = evict("SSSS")
+            inter("V", c, 1)
+            xts = flip(d, ["w0", "w1"])
+            quant_mul(c, 0)
+            inter("V", c, 2)
+            kn = flip_copy(xts, "S")
+            quant_mul(c, 1)
+            if c == 2:
+                load_pair(3, 3)
+            if c == 1:
+                wc.append(quantize(w_ilv[0], "wq", 1, E4))
+            hi = interleave("V", d[:])
+            if c == 2:
+                load_pair(3, 4)
+            xi = interleave("V", x_raw[c - 1][:])
+            inter("S", c, 3)
+            h = quantize(hi, "h", 2, E5)
+            o = dx_mul(h, ["w2", "w3", "w0", "w1"])
+            inter("V", c, 4)
+            kcodes.append(quantize(kn, "k", NB, E5))
+            quant_mul(c, 2)
+            for b in range(4):
+                dx_store(c - 1, b, o[b], "S")
+            quant_x(xi)
+            if c == NB - 1:
+                dw_mul(0, range(NB - 1))
+                dw_mul(1, range(NB - 1))
+            quant_mul(c, 3)
+            if c < NB - 1:
+                inter("S", c + 1, 0)
+            quant_mul(c, 4)
+
+        xi = interleave("V", x_raw[NB - 1][:])
+        d = evict("SVSV")
+        xts = flip(d, ["dh0", "dh1"])
+        dw_mul(2, range(NB - 1))
+        dw_mul(3, range(NB - 1))
+        hi = interleave("V", d[:])
+        kn = flip_copy(xts, "S")
+        quant_x(xi)
+        h = quantize(hi, "h", 2, E5)
+        o = dx_mul(h, ["dh2", "dh3", "dh0", "dh1"])
+        kcodes.append(quantize(kn, "k", NB, E5))
+        for a in range(4):
+            dw_mul(a, [NB - 1])
+        for b in range(4):
+            dx_store(NB - 1, b, o[b], "SV"[b % 2])
+        for a in range(4):
+            t = new([P, HID], F32, "out", 6)
+            copy(
+                "SV"[a % 2],
+                t[:].rearrange("p (m t) -> p m t", t=4),
+                acc[a][:].rearrange("p (t m) -> p m t", t=4),
+            )
+            nc.sync.dma_start(out=out_1[P * a : P * (a + 1), :], in_=t[:])

@@ -20,6 +20,10 @@ MULT = mybir.AluOpType.mult
 P = 128
 B = 512
 NB = N // B
+RUN = 4
+LAST = 352
+XS = 256
+SPLIT = 400
 
 
 def tile_allgnn_pa_v_kernel(tc, x, adj, W_in, b_in, deg, grad_out, out_0, out_1):
@@ -63,43 +67,45 @@ def tile_allgnn_pa_v_kernel(tc, x, adj, W_in, b_in, deg, grad_out, out_0, out_1)
             else:
                 nc.vector.tensor_copy(out=out, in_=in_)
 
-        def interleave(eng, src):
-            dst = new([P, 4 * B], BF16, "ilv", 7)
+        def ilv_tile():
+            return new([P, 4 * B], BF16, "ilv", 7)
+
+        def interleave(eng, dst, src, lo=0, hi=B):
             copy(
                 eng,
-                dst[:].rearrange("p (w i j) -> p w j i", i=4, j=4),
-                src.rearrange("p j (w i) -> p w j i", i=4),
+                dst[:, 4 * lo : 4 * hi].rearrange("p (w i j) -> p w j i", i=RUN, j=4),
+                src[:, :, lo:hi].rearrange("p j (w i) -> p w j i", i=RUN),
             )
-            return dst
 
-        full = slice(0, B)
+        def load(ap, g, c=0):
+            t = new([P, 4, B], BF16, "raw", 22)
+            nc.sync.dma_start(out=t[:], in_=rows(ap, g, slice(B * c, B * (c + 1))))
+            return t
 
         r = new([P, NB, 4], F32, "deg", 1)
-        nc.sync.dma_start(out=r[:], in_=deg.rearrange("(g p j) -> p g j", p=P, j=4))
+        nc.scalar.dma_start(out=r[:], in_=deg.rearrange("(g p j) -> p g j", p=P, j=4))
         ident = new([P, P], F32, "ident", 1)
         make_identity(nc, ident[:])
 
-        def load512(ap, g):
-            t = new([P, 4, B], BF16, "raw512", 11)
-            nc.sync.dma_start(out=t[:], in_=rows(ap, g, full))
-            return t
-
-        graw, araw = [], {}
+        graw, araw, xraw = {}, {}, {}
         w_raw = new([P, 4, HID], BF16, "wraw", 1)
-        for g in range(NB):
-            if g == NB - 1:
-                nc.sync.dma_start(out=w_raw[:], in_=W_in.rearrange("(a p) h -> p a h", p=P))
-            graw.append(load512(grad_out, g))
-            araw[0, g] = load512(adj, g)[:]
 
-        def load_pair(c, g):
-            t = new([P, 4, 2 * B], BF16, "raw1024", 8)
-            nc.sync.dma_start(out=t[:], in_=rows(adj, g, slice(B * c, B * (c + 2))))
-            araw[c, g] = t[:, :, 0:B]
-            araw[c + 1, g] = t[:, :, B : 2 * B]
+        def load_chunk(c):
+            for g in range(1, NB - 1):
+                araw[c, g] = load(adj, g, c)
+            xraw[c - 1] = load(x, c - 1)
+            if c < NB - 1:
+                araw[c + 1, 0] = load(adj, 0, c + 1)
+            araw[c, NB - 1] = load(adj, NB - 1, c)
+            if c == NB - 1:
+                xraw[c] = load(x, c)
 
         for g in range(NB):
-            load_pair(1, g)
+            graw[g] = load(grad_out, g)
+            araw[0, g] = load(adj, g)
+        araw[1, 0] = load(adj, 0, 1)
+        nc.sync.dma_start(out=w_raw[:], in_=W_in.rearrange("(p a) h -> p a h", a=4))
+        load_chunk(1)
 
         nc.vector.tensor_scalar_add(r[:], r[:], 1.0)
         rec = new([P, NB, 4], F32, "rec", 1)
@@ -112,41 +118,47 @@ def tile_allgnn_pa_v_kernel(tc, x, adj, W_in, b_in, deg, grad_out, out_0, out_1)
             return t
 
         def interleave_g(src):
-            dst = new([P, 4 * HID], BF16, "ilv", 7)
+            dst = ilv_tile()
             nc.vector.tensor_copy(
-                out=dst[:].rearrange("p (t m j) -> p t m j", t=4, j=4),
-                in_=src[:].rearrange("p j (m t) -> p t m j", t=4),
+                out=dst[:].rearrange("p (t m j) -> p m j t", t=4, j=4),
+                in_=src[:].rearrange("p j (m t) -> p m j t", t=4),
             )
             return dst
 
         dh = {}
-        gcodes, xcodes, kcodes = [], [], []
-        ailv = {}
+        gcodes, xcodes, kcodes, acodes, ailv = {}, {}, {}, {}, {}
 
-        def inter(eng, c, g):
-            ailv[c, g] = interleave(eng, araw[c, g])
+        def inter(eng, c, g, lo=0, hi=B):
+            if (c, g) not in ailv:
+                ailv[c, g] = ilv_tile()
+            interleave(eng, ailv[c, g], araw[c, g], lo, hi)
 
-        def quant_mul(c, g):
-            a = quantize(ailv[c, g], "a", 4, E4)
+        def quant_a(c, g):
+            acodes[c, g] = quantize(ailv[c, g], "a", 4, E4)
+
+        def dh_mul(c, g):
             for t in range(4):
                 if g == 0:
                     dh[t] = bank("dh" + str(t))
-                mm(dh[t], gcodes[g], slice(P * t, P * (t + 1)), E5, a, E4, g == 0, g == NB - 1)
+                mm(dh[t], gcodes[g], slice(P * t, P * (t + 1)), E5, acodes[c, g], E4, g == 0, g == NB - 1)
 
-        w_words = w_raw[:].bitcast(F32)
-        w_ilv = []
-        wc = []
-
-        def w_transpose():
-            dst = new([P, 4 * IN], BF16, "ilv", 7)
-            dv = dst[:].bitcast(F32).rearrange("p (b a i u) -> p b a i u", b=2, a=2, u=2)
+        def w_flip():
+            w_words = w_raw[:].bitcast(F32)
+            out = []
             for b in range(2):
-                xt = bank("w" + str(b))[:].rearrange("p (a u i) -> p a u i", a=2, u=2)
+                xt = bank("w" + str(2 + b))[:].rearrange("p (a u i) -> p a u i", a=2, u=2)
                 for a in range(2):
                     for u in range(2):
                         nc.tensor.transpose(xt[:, a, u, :], w_words[:, 2 * b + a, u : HID // 2 : 2], ident[:])
-                nc.scalar.copy(out=dv[:, b], in_=xt.rearrange("p a u i -> p a i u"))
-            w_ilv.append(dst)
+                out.append(xt)
+            return out
+
+        def w_copy(xts):
+            dst = ilv_tile()
+            dv = dst[:].bitcast(F32).rearrange("p (i b a u) -> p b i a u", b=2, a=2, u=2)
+            for b in range(2):
+                nc.scalar.copy(out=dv[:, b], in_=xts[b].rearrange("p a u i -> p i a u"))
+            return dst
 
         g2 = scale_g(0)
         inter("S", 0, 0)
@@ -154,121 +166,181 @@ def tile_allgnn_pa_v_kernel(tc, x, adj, W_in, b_in, deg, grad_out, out_0, out_1)
         for g in range(1, NB):
             g2 = scale_g(g)
             inter("S", 0, g)
-            gcodes.append(quantize(gi, "g", NB, E5))
+            gcodes[g - 1] = quantize(gi, "g", NB, E5)
             gi = interleave_g(g2)
-            quant_mul(0, g - 1)
-        x_raw = [load512(x, 0), load512(x, 1)]
-        for g in range(3):
-            load_pair(3, g)
-        for g in range(2, NB):
-            x_raw.append(load512(x, g))
-        gcodes.append(quantize(gi, "g", NB, E5))
-        w_transpose()
+            quant_a(0, g - 1)
+            dh_mul(0, g - 1)
+        load_chunk(2)
         inter("S", 1, 0)
-        quant_mul(0, NB - 1)
+        gcodes[NB - 1] = quantize(gi, "g", NB, E5)
+        w_banks = w_flip()
+        quant_a(0, NB - 1)
+        dh_mul(0, NB - 1)
+        wi = w_copy(w_banks)
+        inter("V", 1, 1)
 
         def evict(engs):
-            d = new([P, 4, B], BF16, "d", 2)
+            d = new([P, 4 * B], BF16, "d", 2)
             for t in range(4):
-                copy(engs[t], d[:, t, :], dh[t][:])
+                copy(
+                    engs[t],
+                    d[:, B * t : B * (t + 1)].rearrange("p (u m e) -> p u m e", u=2, e=2),
+                    dh[t][:].rearrange("p (m u e) -> p u m e", u=2, e=2),
+                )
             return d
 
+        def inter_h(dst, d, u):
+            nc.vector.tensor_copy(
+                out=dst[:, 2 * B * u : 2 * B * (u + 1)].rearrange("p (e m t) -> p m t e", e=2, t=4),
+                in_=d[:].rearrange("p (t u m e) -> p u m t e", t=4, u=2, e=2)[:, u],
+            )
+
+        def inter_h_all(dst, d):
+            nc.vector.tensor_copy(
+                out=dst[:].rearrange("p (u e m t) -> p u m t e", u=2, e=2, t=4),
+                in_=d[:].rearrange("p (t u m e) -> p u m t e", t=4, u=2, e=2),
+            )
+
         def flip(d, tags):
-            words = d[:].bitcast(F32)
             out = []
             for b in range(2):
                 xt = bank(tags[b])[:].rearrange("p (t u m) -> p t u m", t=2, u=2)
                 for t in range(2):
+                    words = d[:, B * (2 * b + t) : B * (2 * b + t + 1)].bitcast(F32)
                     for u in range(2):
-                        nc.tensor.transpose(xt[:, t, u, :], words[:, 2 * b + t, u : B // 2 : 2], ident[:])
+                        nc.tensor.transpose(xt[:, t, u, :], words[:, P * u : P * (u + 1)], ident[:])
                 out.append(xt)
             return out
 
-        def flip_copy(xts, eng):
-            dst = new([P, 4 * HID], BF16, "ilv", 7)
+        def flip_copy(xts, engs):
+            dst = ilv_tile()
             dv = dst[:].bitcast(F32).rearrange("p (b t m u) -> p b t m u", b=2, t=2, u=2)
             for b in range(2):
-                copy(eng, dv[:, b], xts[b].rearrange("p t u m -> p t m u"))
+                copy(engs[b], dv[:, b], xts[b].rearrange("p t u m -> p t m u"))
             return dst
 
-        def dx_mul(h, tags):
-            out = []
-            for b in range(4):
-                o = bank(tags[b])
-                mm(o, h, slice(P * b, P * (b + 1)), E5, wc[0], E4, True, True)
-                out.append(o)
-            return out
+        def dx_mul(h, b, tag):
+            o = bank(tag)
+            mm(o, h, slice(P * b, P * (b + 1)), E5, wcodes[0], E4, True, True)
+            return o
 
         def dx_store(c, b, o, eng):
-            t = new([P, IN], F32, "out", 6)
+            t = new([P, IN], F32, "out", 14)
             copy(eng, t[:], o[:])
-            n0 = B * c + P * b
-            nc.sync.dma_start(out=out_0[n0 : n0 + P, :], in_=t[:])
+            nc.sync.dma_start(out=rows(out_0, c, slice(0, IN))[:, b, :], in_=t[:])
 
-        acc = {}
+        acc, wcodes = {}, []
 
-        def dw_mul(a, cs):
-            for c in cs:
-                if c == 0:
-                    acc[a] = bank("w" + str((a + 2) % 4))
-                mm(acc[a], xcodes[c], slice(P * a, P * (a + 1)), E4, kcodes[c], E5, c == 0, c == NB - 1)
+        def dw_mul(a, c):
+            if c == 0:
+                acc[a] = bank("w" + str((a + 2) % 4))
+            mm(acc[a], xcodes[c], slice(P * a, P * (a + 1)), E4, kcodes[c], E5, c == 0, c == NB - 1)
 
-        def quant_x(src):
-            xcodes.append(quantize(src, "x", NB, E4))
-
-        for c in range(1, NB):
-            d = evict("SSSS")
-            inter("V", c, 1)
-            xts = flip(d, ["w0", "w1"])
-            quant_mul(c, 0)
-            inter("V", c, 2)
-            kn = flip_copy(xts, "S")
-            quant_mul(c, 1)
-            if c == 2:
-                load_pair(3, 3)
-            if c == 1:
-                wc.append(quantize(w_ilv[0], "wq", 1, E4))
-            hi = interleave("V", d[:])
-            if c == 2:
-                load_pair(3, 4)
-            xi = interleave("V", x_raw[c - 1][:])
-            inter("S", c, 3)
-            h = quantize(hi, "h", 2, E5)
-            o = dx_mul(h, ["w2", "w3", "w0", "w1"])
-            inter("V", c, 4)
-            kcodes.append(quantize(kn, "k", NB, E5))
-            quant_mul(c, 2)
-            for b in range(4):
-                dx_store(c - 1, b, o[b], "S")
-            quant_x(xi)
-            if c == NB - 1:
-                dw_mul(0, range(NB - 1))
-                dw_mul(1, range(NB - 1))
-            quant_mul(c, 3)
-            if c < NB - 1:
-                inter("S", c + 1, 0)
-            quant_mul(c, 4)
-
-        xi = interleave("V", x_raw[NB - 1][:])
-        d = evict("SVSV")
-        xts = flip(d, ["dh0", "dh1"])
-        dw_mul(2, range(NB - 1))
-        dw_mul(3, range(NB - 1))
-        hi = interleave("V", d[:])
-        kn = flip_copy(xts, "S")
-        quant_x(xi)
-        h = quantize(hi, "h", 2, E5)
-        o = dx_mul(h, ["dh2", "dh3", "dh0", "dh1"])
-        kcodes.append(quantize(kn, "k", NB, E5))
-        for a in range(4):
-            dw_mul(a, [NB - 1])
-        for b in range(4):
-            dx_store(NB - 1, b, o[b], "SV"[b % 2])
-        for a in range(4):
-            t = new([P, HID], F32, "out", 6)
+        def dw_store(a, eng):
+            t = new([P, HID], F32, "out", 14)
             copy(
-                "SV"[a % 2],
+                eng,
                 t[:].rearrange("p (m t) -> p m t", t=4),
                 acc[a][:].rearrange("p (t m) -> p m t", t=4),
             )
             nc.sync.dma_start(out=out_1[P * a : P * (a + 1), :], in_=t[:])
+
+        def inter_x(eng, c):
+            t = ilv_tile()
+            interleave(eng, t, xraw[c])
+            return t
+
+        def front(c):
+            d = evict("SSSS")
+            quant_a(c, 0)
+            dh_mul(c, 0)
+            xts = flip(d, ["w0", "w1"])
+            inter("V", c, 2)
+            quant_a(c, 1)
+            dh_mul(c, 1)
+            inter("S", c, 3)
+            hi = ilv_tile()
+            inter_h_all(hi, d)
+            quant_a(c, 2)
+            kn = flip_copy(xts, "SS")
+            dh_mul(c, 2)
+            return quantize(hi, "h", 2, E5), kn
+
+        for c in range(1, NB - 1):
+            h, kn = front(c)
+            if c == 1:
+                wcodes.append(quantize(wi, "wq", 1, E4))
+            xi = inter_x("V", c - 1)
+            o = [dx_mul(h, b, "w" + str(b)) for b in range(2)]
+            if c + 2 < NB:
+                load_chunk(c + 2)
+            inter("S", c + 1, 0, 0, B // 2)
+            quant_a(c, 3)
+            inter("V", c, 4)
+            for b in range(2):
+                dx_store(c - 1, b, o[b], "S")
+            dh_mul(c, 3)
+            o = [dx_mul(h, b + 2, "w" + str(b)) for b in range(2)]
+            inter("S", c + 1, 0, B // 2, B)
+            kcodes[c - 1] = quantize(kn, "k", NB, E5)
+            quant_a(c, 4)
+            dh_mul(c, 4)
+            xcodes[c - 1] = quantize(xi, "x", NB, E4)
+            dw_mul(0, c - 1)
+            dw_mul(1, c - 1)
+            for b in range(2):
+                dx_store(c - 1, b + 2, o[b], "S")
+            inter("S", c + 1, 1, SPLIT, B)
+            inter("V", c + 1, 1, 0, SPLIT)
+
+        c = NB - 1
+        H = B // 2
+        h, kn = front(c)
+        o = [dx_mul(h, b, "w" + str(b)) for b in range(2)]
+        quant_a(c, 3)
+        inter("S", c, 4, LAST, B)
+        inter("V", c, 4, 0, LAST)
+        for b in range(2):
+            dx_store(c - 1, b, o[b], "S")
+        dh_mul(c, 3)
+        kcodes[c - 1] = quantize(kn, "k", NB, E5)
+        quant_a(c, 4)
+        o2 = dx_mul(h, 2, "w0")
+        dh_mul(c, 4)
+        o3 = dx_mul(h, 3, "w1")
+        dx_store(c - 1, 2, o2, "S")
+        xi = inter_x("V", c - 1)
+        d = evict("SVSV")
+        dx_store(c - 1, 3, o3, "S")
+        dw_mul(2, 0)
+        xts = flip(d, ["dh0", "dh1"])
+        for k in range(1, NB - 2):
+            dw_mul(2, k)
+        for k in range(NB - 2):
+            dw_mul(3, k)
+        hi = ilv_tile()
+        hc, hs = codes("h", 2)
+        xl = ilv_tile()
+        kn = flip_copy(xts, "SS")
+
+        def dx_half(u):
+            cols = slice(H * u, H * (u + 1))
+            nc.vector.quantize_mx(out=hc[:, cols].bitcast(E5), scales=hs[:, cols], in_=hi[:, 4 * H * u : 4 * H * (u + 1)])
+            return [dx_mul((hc, hs), b, "dh" + str((b + 2) % 4)) for b in (2 * u, 2 * u + 1)]
+
+        inter_h(hi, d, 0)
+        inter_h(hi, d, 1)
+        o = dx_half(0) + dx_half(1)
+        xcodes[c - 1] = quantize(xi, "x", NB, E4)
+        for a in range(4):
+            dw_mul(a, c - 1)
+        interleave("S", xl, xraw[c], XS, B)
+        interleave("V", xl, xraw[c], 0, XS)
+        kcodes[c] = quantize(kn, "k", NB, E5)
+        for b in range(4):
+            dx_store(c, b, o[b], "S")
+        xcodes[c] = quantize(xl, "x", NB, E4)
+        for a in range(4):
+            dw_mul(a, c)
+        for a in range(4):
+            dw_store(a, "SV"[a % 2])

@@ -21,8 +21,10 @@ P = 128
 B = 512
 NB = N // B
 RUN = 4
+HEAD = 256
+FIRST = 320
 LAST = 352
-XS = 256
+XV = 384
 SPLIT = 400
 
 
@@ -93,6 +95,8 @@ def tile_allgnn_pa_v_kernel(tc, x, adj, W_in, b_in, deg, grad_out, out_0, out_1)
         def load_chunk(c):
             for g in range(1, NB - 1):
                 araw[c, g] = load(adj, g, c)
+                if (c, g) == (1, 1):
+                    nc.sync.dma_start(out=w_raw[:], in_=W_in.rearrange("(p a) h -> p a h", a=4))
             xraw[c - 1] = load(x, c - 1)
             if c < NB - 1:
                 araw[c + 1, 0] = load(adj, 0, c + 1)
@@ -100,11 +104,14 @@ def tile_allgnn_pa_v_kernel(tc, x, adj, W_in, b_in, deg, grad_out, out_0, out_1)
             if c == NB - 1:
                 xraw[c] = load(x, c)
 
+        graw[0] = new([P, 4, B], BF16, "raw", 22)
+        for j in (0, 2):
+            nc.sync.dma_start(out=graw[0][:, j : j + 2, :], in_=rows(grad_out, 0, slice(0, HID))[:, j : j + 2, :])
         for g in range(NB):
-            graw[g] = load(grad_out, g)
+            if g + 1 < NB:
+                graw[g + 1] = load(grad_out, g + 1)
             araw[0, g] = load(adj, g)
         araw[1, 0] = load(adj, 0, 1)
-        nc.sync.dma_start(out=w_raw[:], in_=W_in.rearrange("(p a) h -> p a h", a=4))
         load_chunk(1)
 
         nc.vector.tensor_scalar_add(r[:], r[:], 1.0)
@@ -117,7 +124,14 @@ def tile_allgnn_pa_v_kernel(tc, x, adj, W_in, b_in, deg, grad_out, out_0, out_1)
                 nc.vector.tensor_scalar_mul(t[:, j, :], graw[g][:, j, :], rec[:, g, j : j + 1])
             return t
 
-        def interleave_g(src):
+        def interleave_g(eng, dst, src, u):
+            copy(
+                eng,
+                dst[:, 2 * HID * u : 2 * HID * (u + 1)].rearrange("p (e m j) -> p m j e", e=2, j=4),
+                src[:].rearrange("p j (m u e) -> p u m j e", u=2, e=2)[:, u],
+            )
+
+        def interleave_g_all(src):
             dst = ilv_tile()
             nc.vector.tensor_copy(
                 out=dst[:].rearrange("p (t m j) -> p m j t", t=4, j=4),
@@ -161,23 +175,28 @@ def tile_allgnn_pa_v_kernel(tc, x, adj, W_in, b_in, deg, grad_out, out_0, out_1)
             return dst
 
         g2 = scale_g(0)
-        inter("S", 0, 0)
-        gi = interleave_g(g2)
+        gi = ilv_tile()
+        interleave_g("V", gi, g2, 0)
+        interleave_g("S", gi, g2, 1)
         for g in range(1, NB):
             g2 = scale_g(g)
-            inter("S", 0, g)
+            inter("S", 0, g - 1)
             gcodes[g - 1] = quantize(gi, "g", NB, E5)
-            gi = interleave_g(g2)
-            quant_a(0, g - 1)
-            dh_mul(0, g - 1)
+            gi = interleave_g_all(g2)
+            if g > 1:
+                quant_a(0, g - 2)
+                dh_mul(0, g - 2)
+        inter("S", 0, NB - 1, HEAD, B)
+        inter("V", 0, NB - 1, 0, HEAD)
+        quant_a(0, NB - 2)
+        dh_mul(0, NB - 2)
         load_chunk(2)
         inter("S", 1, 0)
         gcodes[NB - 1] = quantize(gi, "g", NB, E5)
-        w_banks = w_flip()
         quant_a(0, NB - 1)
         dh_mul(0, NB - 1)
-        wi = w_copy(w_banks)
         inter("V", 1, 1)
+        w_banks = w_flip()
 
         def evict(engs):
             d = new([P, 4 * B], BF16, "d", 2)
@@ -229,7 +248,7 @@ def tile_allgnn_pa_v_kernel(tc, x, adj, W_in, b_in, deg, grad_out, out_0, out_1)
             copy(eng, t[:], o[:])
             nc.sync.dma_start(out=rows(out_0, c, slice(0, IN))[:, b, :], in_=t[:])
 
-        acc, wcodes = {}, []
+        acc, wcodes, w_ilv = {}, [], []
 
         def dw_mul(a, c):
             if c == 0:
@@ -252,6 +271,8 @@ def tile_allgnn_pa_v_kernel(tc, x, adj, W_in, b_in, deg, grad_out, out_0, out_1)
 
         def front(c):
             d = evict("SSSS")
+            if c == 1:
+                w_ilv.append(w_copy(w_banks))
             quant_a(c, 0)
             dh_mul(c, 0)
             xts = flip(d, ["w0", "w1"])
@@ -269,19 +290,20 @@ def tile_allgnn_pa_v_kernel(tc, x, adj, W_in, b_in, deg, grad_out, out_0, out_1)
         for c in range(1, NB - 1):
             h, kn = front(c)
             if c == 1:
-                wcodes.append(quantize(wi, "wq", 1, E4))
+                wcodes.append(quantize(w_ilv[0], "wq", 1, E4))
             xi = inter_x("V", c - 1)
             o = [dx_mul(h, b, "w" + str(b)) for b in range(2)]
             if c + 2 < NB:
                 load_chunk(c + 2)
-            inter("S", c + 1, 0, 0, B // 2)
+            inter("S", c + 1, 0, 0, FIRST)
             quant_a(c, 3)
             inter("V", c, 4)
             for b in range(2):
                 dx_store(c - 1, b, o[b], "S")
             dh_mul(c, 3)
             o = [dx_mul(h, b + 2, "w" + str(b)) for b in range(2)]
-            inter("S", c + 1, 0, B // 2, B)
+            inter("S", c + 1, 0, FIRST, B)
+            inter("S", c + 1, 1, SPLIT, B)
             kcodes[c - 1] = quantize(kn, "k", NB, E5)
             quant_a(c, 4)
             dh_mul(c, 4)
@@ -290,7 +312,6 @@ def tile_allgnn_pa_v_kernel(tc, x, adj, W_in, b_in, deg, grad_out, out_0, out_1)
             dw_mul(1, c - 1)
             for b in range(2):
                 dx_store(c - 1, b + 2, o[b], "S")
-            inter("S", c + 1, 1, SPLIT, B)
             inter("V", c + 1, 1, 0, SPLIT)
 
         c = NB - 1
@@ -309,38 +330,69 @@ def tile_allgnn_pa_v_kernel(tc, x, adj, W_in, b_in, deg, grad_out, out_0, out_1)
         dh_mul(c, 4)
         o3 = dx_mul(h, 3, "w1")
         dx_store(c - 1, 2, o2, "S")
-        xi = inter_x("V", c - 1)
-        d = evict("SVSV")
-        dx_store(c - 1, 3, o3, "S")
-        dw_mul(2, 0)
-        xts = flip(d, ["dh0", "dh1"])
-        for k in range(1, NB - 2):
-            dw_mul(2, k)
-        for k in range(NB - 2):
-            dw_mul(3, k)
+        xi = ilv_tile()
+        interleave("V", xi, xraw[c - 1], 0, XV)
+        d = new([P, 4 * B], BF16, "d", 2)
+
+        def evict_half(u, engs):
+            for t in range(4):
+                copy(
+                    engs[t],
+                    d[:, B * t + H * u : B * t + H * (u + 1)].rearrange("p (m e) -> p m e", e=2),
+                    dh[t][:].rearrange("p (m u e) -> p u m e", u=2, e=2)[:, u],
+                )
+
         hi = ilv_tile()
         hc, hs = codes("h", 2)
-        xl = ilv_tile()
-        kn = flip_copy(xts, "SS")
 
         def dx_half(u):
             cols = slice(H * u, H * (u + 1))
             nc.vector.quantize_mx(out=hc[:, cols].bitcast(E5), scales=hs[:, cols], in_=hi[:, 4 * H * u : 4 * H * (u + 1)])
             return [dx_mul((hc, hs), b, "dh" + str((b + 2) % 4)) for b in (2 * u, 2 * u + 1)]
 
-        inter_h(hi, d, 0)
-        inter_h(hi, d, 1)
-        o = dx_half(0) + dx_half(1)
-        xcodes[c - 1] = quantize(xi, "x", NB, E4)
-        for a in range(4):
-            dw_mul(a, c - 1)
-        interleave("S", xl, xraw[c], XS, B)
-        interleave("V", xl, xraw[c], 0, XS)
-        kcodes[c] = quantize(kn, "k", NB, E5)
-        for b in range(4):
-            dx_store(c, b, o[b], "S")
-        xcodes[c] = quantize(xl, "x", NB, E4)
-        for a in range(4):
+        xl = ilv_tile()
+        xcodes[c] = codes("x", NB)
+
+        def x_part(eng, a):
+            interleave(eng, xl, xraw[c], P * a, P * (a + 1))
+
+        def dw_last(a):
+            xc, xs = xcodes[c]
+            cols = slice(P * a, P * (a + 1))
+            nc.vector.quantize_mx(out=xc[:, cols].bitcast(E4), scales=xs[:, cols], in_=xl[:, B * a : B * (a + 1)])
             dw_mul(a, c)
-        for a in range(4):
-            dw_store(a, "SV"[a % 2])
+
+        evict_half(0, "SVSV")
+        evict_half(1, "SSSS")
+        interleave("V", xi, xraw[c - 1], XV, B)
+        inter_h(hi, d, 0)
+        dx_store(c - 1, 3, o3, "S")
+        dw_mul(2, 0)
+        xts = flip(d, ["dh0", "dh1"])
+        kn = flip_copy(xts, "SS")
+        for k in range(1, NB - 2):
+            dw_mul(2, k)
+        x_part("V", 0)
+        o = dx_half(0)
+        inter_h(hi, d, 1)
+        xcodes[c - 1] = quantize(xi, "x", NB, E4)
+        for k in range(NB - 2):
+            dw_mul(3, k)
+        o.extend(dx_half(1))
+        for b in range(2):
+            dx_store(c, b, o[b], "S")
+        kcodes[c] = quantize(kn, "k", NB, E5)
+        dw_mul(0, c - 1)
+        dw_last(0)
+        x_part("V", 1)
+        x_part("S", 3)
+        dx_store(c, 2, o[2], "S")
+        x_part("V", 2)
+        for a in range(1, 4):
+            dw_mul(a, c - 1)
+        for a in range(1, 4):
+            dw_last(a)
+        dx_store(c, 3, o[3], "S")
+        dw_store(0, "V")
+        for a in range(1, 4):
+            dw_store(a, "SV"[(a + 1) % 2])

@@ -20,7 +20,7 @@ MULT = mybir.AluOpType.mult
 P = 128
 B = 512
 NB = N // B
-RUN = 4
+RUN = 8
 HEAD = 256
 FIRST = 320
 LAST = 352
@@ -75,8 +75,8 @@ def tile_allgnn_pa_v_kernel(tc, x, adj, W_in, b_in, deg, grad_out, out_0, out_1)
         def interleave(eng, dst, src, lo=0, hi=B):
             copy(
                 eng,
-                dst[:, 4 * lo : 4 * hi].rearrange("p (w i j) -> p w j i", i=RUN, j=4),
-                src[:, :, lo:hi].rearrange("p j (w i) -> p w j i", i=RUN),
+                dst[:, 4 * lo : 4 * hi].rearrange("p (w i u e) -> p w u i e", i=RUN, u=2, e=2),
+                src[:, :, lo:hi].rearrange("p (u e) (w i) -> p w u i e", i=RUN, u=2),
             )
 
         def load(ap, g, c=0):
@@ -93,14 +93,13 @@ def tile_allgnn_pa_v_kernel(tc, x, adj, W_in, b_in, deg, grad_out, out_0, out_1)
         w_raw = new([P, 4, HID], BF16, "wraw", 1)
 
         def load_chunk(c):
-            for g in range(1, NB - 1):
+            for g in range(1, NB):
                 araw[c, g] = load(adj, g, c)
                 if (c, g) == (1, 1):
                     nc.sync.dma_start(out=w_raw[:], in_=W_in.rearrange("(p a) h -> p a h", a=4))
-            xraw[c - 1] = load(x, c - 1)
             if c < NB - 1:
                 araw[c + 1, 0] = load(adj, 0, c + 1)
-            araw[c, NB - 1] = load(adj, NB - 1, c)
+            xraw[c - 1] = load(x, c - 1)
             if c == NB - 1:
                 xraw[c] = load(x, c)
 
@@ -291,22 +290,22 @@ def tile_allgnn_pa_v_kernel(tc, x, adj, W_in, b_in, deg, grad_out, out_0, out_1)
             h, kn = front(c)
             if c == 1:
                 wcodes.append(quantize(w_ilv[0], "wq", 1, E4))
-            xi = inter_x("V", c - 1)
+            inter("V", c, 4)
             o = [dx_mul(h, b, "w" + str(b)) for b in range(2)]
             if c + 2 < NB:
                 load_chunk(c + 2)
             inter("S", c + 1, 0, 0, FIRST)
             quant_a(c, 3)
-            inter("V", c, 4)
+            quant_a(c, 4)
+            xi = inter_x("V", c - 1)
             for b in range(2):
                 dx_store(c - 1, b, o[b], "S")
             dh_mul(c, 3)
             o = [dx_mul(h, b + 2, "w" + str(b)) for b in range(2)]
+            dh_mul(c, 4)
             inter("S", c + 1, 0, FIRST, B)
             inter("S", c + 1, 1, SPLIT, B)
             kcodes[c - 1] = quantize(kn, "k", NB, E5)
-            quant_a(c, 4)
-            dh_mul(c, 4)
             xcodes[c - 1] = quantize(xi, "x", NB, E4)
             dw_mul(0, c - 1)
             dw_mul(1, c - 1)
@@ -367,28 +366,29 @@ def tile_allgnn_pa_v_kernel(tc, x, adj, W_in, b_in, deg, grad_out, out_0, out_1)
         interleave("V", xi, xraw[c - 1], XV, B)
         inter_h(hi, d, 0)
         dx_store(c - 1, 3, o3, "S")
-        dw_mul(2, 0)
+        for k in range(NB - 2):
+            dw_mul(2, k)
         xts = flip(d, ["dh0", "dh1"])
         kn = flip_copy(xts, "SS")
-        for k in range(1, NB - 2):
-            dw_mul(2, k)
+        dw_mul(3, 0)
         x_part("V", 0)
         o = dx_half(0)
         inter_h(hi, d, 1)
         xcodes[c - 1] = quantize(xi, "x", NB, E4)
-        for k in range(NB - 2):
+        for k in range(1, NB - 2):
             dw_mul(3, k)
+        dw_mul(0, c - 1)
         o.extend(dx_half(1))
         for b in range(2):
             dx_store(c, b, o[b], "S")
         kcodes[c] = quantize(kn, "k", NB, E5)
-        dw_mul(0, c - 1)
+        dw_mul(1, c - 1)
         dw_last(0)
         x_part("V", 1)
         x_part("S", 3)
         dx_store(c, 2, o[2], "S")
         x_part("V", 2)
-        for a in range(1, 4):
+        for a in range(2, 4):
             dw_mul(a, c - 1)
         for a in range(1, 4):
             dw_last(a)

@@ -21,11 +21,10 @@ P = 128
 B = 512
 NB = N // B
 RUN = 8
-HEAD = 256
+HEAD = 320
 FIRST = 320
-LAST = 352
+LAST = 288
 XV = 384
-SPLIT = 400
 
 
 def tile_allgnn_pa_v_kernel(tc, x, adj, W_in, b_in, deg, grad_out, out_0, out_1):
@@ -85,7 +84,7 @@ def tile_allgnn_pa_v_kernel(tc, x, adj, W_in, b_in, deg, grad_out, out_0, out_1)
             return t
 
         r = new([P, NB, 4], F32, "deg", 1)
-        nc.scalar.dma_start(out=r[:], in_=deg.rearrange("(g p j) -> p g j", p=P, j=4))
+        nc.sync.dma_start(out=r[:], in_=deg.rearrange("(g p j) -> p g j", p=P, j=4))
         ident = new([P, P], F32, "ident", 1)
         make_identity(nc, ident[:])
 
@@ -106,9 +105,10 @@ def tile_allgnn_pa_v_kernel(tc, x, adj, W_in, b_in, deg, grad_out, out_0, out_1)
         graw[0] = new([P, 4, B], BF16, "raw", 22)
         for j in (0, 2):
             nc.sync.dma_start(out=graw[0][:, j : j + 2, :], in_=rows(grad_out, 0, slice(0, HID))[:, j : j + 2, :])
+        graw[1] = load(grad_out, 1)
         for g in range(NB):
-            if g + 1 < NB:
-                graw[g + 1] = load(grad_out, g + 1)
+            if g + 2 < NB:
+                graw[g + 2] = load(grad_out, g + 2)
             araw[0, g] = load(adj, g)
         araw[1, 0] = load(adj, 0, 1)
         load_chunk(1)
@@ -118,7 +118,7 @@ def tile_allgnn_pa_v_kernel(tc, x, adj, W_in, b_in, deg, grad_out, out_0, out_1)
         nc.vector.reciprocal(out=rec[:], in_=r[:])
 
         def scale_g(g):
-            t = new([P, 4, HID], BF16, "g2", 2)
+            t = new([P, 4, HID], BF16, "g2", 3)
             for j in range(4):
                 nc.vector.tensor_scalar_mul(t[:, j, :], graw[g][:, j, :], rec[:, g, j : j + 1])
             return t
@@ -130,11 +130,12 @@ def tile_allgnn_pa_v_kernel(tc, x, adj, W_in, b_in, deg, grad_out, out_0, out_1)
                 src[:].rearrange("p j (m u e) -> p u m j e", u=2, e=2)[:, u],
             )
 
-        def interleave_g_all(src):
+        def interleave_g_all(eng, src):
             dst = ilv_tile()
-            nc.vector.tensor_copy(
-                out=dst[:].rearrange("p (t m j) -> p m j t", t=4, j=4),
-                in_=src[:].rearrange("p j (m t) -> p m j t", t=4),
+            copy(
+                eng,
+                dst[:].rearrange("p (t m j) -> p m j t", t=4, j=4),
+                src[:].rearrange("p j (m t) -> p m j t", t=4),
             )
             return dst
 
@@ -173,27 +174,42 @@ def tile_allgnn_pa_v_kernel(tc, x, adj, W_in, b_in, deg, grad_out, out_0, out_1)
                 nc.scalar.copy(out=dv[:, b], in_=xts[b].rearrange("p a u i -> p i a u"))
             return dst
 
+        def quant_g(g):
+            gcodes[g] = quantize(gi[g], "g", NB, E5)
+
+        def head_pass(g):
+            quant_a(0, g)
+            dh_mul(0, g)
+
+        gi = {0: ilv_tile()}
         g2 = scale_g(0)
-        gi = ilv_tile()
-        interleave_g("V", gi, g2, 0)
-        interleave_g("S", gi, g2, 1)
-        for g in range(1, NB):
-            g2 = scale_g(g)
-            inter("S", 0, g - 1)
-            gcodes[g - 1] = quantize(gi, "g", NB, E5)
-            gi = interleave_g_all(g2)
-            if g > 1:
-                quant_a(0, g - 2)
-                dh_mul(0, g - 2)
-        inter("S", 0, NB - 1, HEAD, B)
-        inter("V", 0, NB - 1, 0, HEAD)
-        quant_a(0, NB - 2)
-        dh_mul(0, NB - 2)
+        interleave_g("V", gi[0], g2, 0)
+        interleave_g("S", gi[0], g2, 1)
+        gi[1] = interleave_g_all("S", scale_g(1))
+        g2 = scale_g(2)
+        quant_g(0)
+        gi[2] = interleave_g_all("V", g2)
+        inter("S", 0, 0)
+        g2 = scale_g(3)
+        quant_g(1)
+        gi[3] = interleave_g_all("V", g2)
+        inter("S", 0, 1)
+        head_pass(0)
+        g2 = scale_g(4)
+        quant_g(2)
+        head_pass(1)
+        gi[4] = interleave_g_all("V", g2)
+        inter("S", 0, 2)
+        quant_g(3)
+        inter("S", 0, 3)
+        head_pass(2)
+        quant_g(4)
+        inter("S", 0, 4, HEAD, B)
+        inter("V", 0, 4, 0, HEAD)
         load_chunk(2)
         inter("S", 1, 0)
-        gcodes[NB - 1] = quantize(gi, "g", NB, E5)
-        quant_a(0, NB - 1)
-        dh_mul(0, NB - 1)
+        head_pass(3)
+        head_pass(4)
         inter("V", 1, 1)
         w_banks = w_flip()
 
@@ -243,7 +259,7 @@ def tile_allgnn_pa_v_kernel(tc, x, adj, W_in, b_in, deg, grad_out, out_0, out_1)
             return o
 
         def dx_store(c, b, o, eng):
-            t = new([P, IN], F32, "out", 14)
+            t = new([P, IN], F32, "out", 12)
             copy(eng, t[:], o[:])
             nc.sync.dma_start(out=rows(out_0, c, slice(0, IN))[:, b, :], in_=t[:])
 
@@ -255,7 +271,7 @@ def tile_allgnn_pa_v_kernel(tc, x, adj, W_in, b_in, deg, grad_out, out_0, out_1)
             mm(acc[a], xcodes[c], slice(P * a, P * (a + 1)), E4, kcodes[c], E5, c == 0, c == NB - 1)
 
         def dw_store(a, eng):
-            t = new([P, HID], F32, "out", 14)
+            t = new([P, HID], F32, "out", 12)
             copy(
                 eng,
                 t[:].rearrange("p (m t) -> p m t", t=4),
@@ -304,14 +320,13 @@ def tile_allgnn_pa_v_kernel(tc, x, adj, W_in, b_in, deg, grad_out, out_0, out_1)
             o = [dx_mul(h, b + 2, "w" + str(b)) for b in range(2)]
             dh_mul(c, 4)
             inter("S", c + 1, 0, FIRST, B)
-            inter("S", c + 1, 1, SPLIT, B)
             kcodes[c - 1] = quantize(kn, "k", NB, E5)
             xcodes[c - 1] = quantize(xi, "x", NB, E4)
             dw_mul(0, c - 1)
             dw_mul(1, c - 1)
             for b in range(2):
                 dx_store(c - 1, b + 2, o[b], "S")
-            inter("V", c + 1, 1, 0, SPLIT)
+            inter("V", c + 1, 1)
 
         c = NB - 1
         H = B // 2

@@ -15,16 +15,14 @@ U32 = mybir.dt.uint32
 U8 = mybir.dt.uint8
 E4 = mybir.dt.float8_e4m3fn_x4
 E5 = mybir.dt.float8_e5m2_x4
-MULT = mybir.AluOpType.mult
 
 P = 128
 B = 512
 NB = N // B
+H = B // 2
 RUN = 8
-HEAD = 320
-FIRST = 320
-LAST = 288
-XV = 384
+HEAD = 384
+X2S = 320
 
 
 def tile_allgnn_pa_v_kernel(tc, x, adj, W_in, b_in, deg, grad_out, out_0, out_1):
@@ -40,21 +38,33 @@ def tile_allgnn_pa_v_kernel(tc, x, adj, W_in, b_in, deg, grad_out, out_0, out_1)
         def bank(tag):
             return ps.tile([P, B], F32, tag=tag, name=tag, bufs=1)
 
-        def codes(tag, bufs):
-            return new([P, B], U32, tag + "c", bufs), new([P, B], U8, tag + "s", bufs)
+        def codes(tag, bufs, n):
+            return new([P, n * B], U32, tag + "c", bufs), new([P, n * B], U8, tag + "s", bufs)
 
-        def quantize(src, tag, bufs, fmt):
-            c, s = codes(tag, bufs)
-            nc.vector.quantize_mx(out=c[:].bitcast(fmt), scales=s[:], in_=src[:])
-            return c, s
+        def quant(dst, src, fmt):
+            nc.vector.quantize_mx(out=dst[0].bitcast(fmt), scales=dst[1], in_=src)
 
-        def mm(out, l, lcols, lfmt, r, rfmt, start, stop):
+        def part(cs, lo, hi):
+            return cs[0][:, lo:hi], cs[1][:, lo:hi]
+
+        def quant1(src, tag, bufs, fmt):
+            cs = part(codes(tag, bufs, 1), 0, B)
+            quant(cs, src, fmt)
+            return cs
+
+        def quant2(src, tag, bufs, fmt):
+            cs = codes(tag, bufs, 2)
+            quant(part(cs, 0, 2 * B), src[:], fmt)
+            return part(cs, 0, B), part(cs, B, 2 * B)
+
+        def mm(out, l, blk, lfmt, r, rfmt, start, stop):
+            cols = slice(P * blk, P * (blk + 1))
             nc.tensor.matmul_mx(
                 out=out[:],
-                lhsT=l[0][:, lcols].bitcast(lfmt),
-                lhsT_scale=l[1][:, lcols],
-                rhs=r[0][:].bitcast(rfmt),
-                rhs_scale=r[1][:],
+                lhsT=l[0][:, cols].bitcast(lfmt),
+                lhsT_scale=l[1][:, cols],
+                rhs=r[0].bitcast(rfmt),
+                rhs_scale=r[1],
                 start=start,
                 stop=stop,
             )
@@ -68,10 +78,13 @@ def tile_allgnn_pa_v_kernel(tc, x, adj, W_in, b_in, deg, grad_out, out_0, out_1)
             else:
                 nc.vector.tensor_copy(out=out, in_=in_)
 
-        def ilv_tile():
-            return new([P, 4 * B], BF16, "ilv", 7)
+        def pair():
+            return new([P, 8 * B], BF16, "ilv", 6)
 
-        def interleave(eng, dst, src, lo=0, hi=B):
+        def half(t, i):
+            return t[:, 4 * B * i : 4 * B * (i + 1)]
+
+        def interleave(eng, dst, src, lo, hi):
             copy(
                 eng,
                 dst[:, 4 * lo : 4 * hi].rearrange("p (w i u e) -> p w u i e", i=RUN, u=2, e=2),
@@ -79,199 +92,178 @@ def tile_allgnn_pa_v_kernel(tc, x, adj, W_in, b_in, deg, grad_out, out_0, out_1)
             )
 
         def load(ap, g, c=0):
-            t = new([P, 4, B], BF16, "raw", 22)
+            t = new([P, 4, B], BF16, "raw", 12)
             nc.sync.dma_start(out=t[:], in_=rows(ap, g, slice(B * c, B * (c + 1))))
             return t
+
+        def load2(a, b):
+            t = new([P, 4, 2 * B], BF16, "raw2", 4)
+            nc.sync.dma_start(out=t[:, :, :B], in_=a)
+            nc.sync.dma_start(out=t[:, :, B:], in_=b)
+            return t
+
+        def adj_rows(g, c):
+            return rows(adj, g, slice(B * c, B * (c + 1)))
 
         r = new([P, NB, 4], F32, "deg", 1)
         nc.sync.dma_start(out=r[:], in_=deg.rearrange("(g p j) -> p g j", p=P, j=4))
         ident = new([P, P], F32, "ident", 1)
         make_identity(nc, ident[:])
 
-        graw, araw, xraw = {}, {}, {}
-        w_raw = new([P, 4, HID], BF16, "wraw", 1)
-
-        def load_chunk(c):
-            for g in range(1, NB):
-                araw[c, g] = load(adj, g, c)
-                if (c, g) == (1, 1):
-                    nc.sync.dma_start(out=w_raw[:], in_=W_in.rearrange("(p a) h -> p a h", a=4))
-            if c < NB - 1:
-                araw[c + 1, 0] = load(adj, 0, c + 1)
-            xraw[c - 1] = load(x, c - 1)
-            if c == NB - 1:
-                xraw[c] = load(x, c)
-
-        graw[0] = new([P, 4, B], BF16, "raw", 22)
+        graw, a0raw, first, second, last, xraw = {}, {}, {}, {}, {}, {}
+        graw[0] = new([P, 4, B], BF16, "raw", 12)
         for j in (0, 2):
             nc.sync.dma_start(out=graw[0][:, j : j + 2, :], in_=rows(grad_out, 0, slice(0, HID))[:, j : j + 2, :])
         graw[1] = load(grad_out, 1)
         for g in range(NB):
             if g + 2 < NB:
                 graw[g + 2] = load(grad_out, g + 2)
-            araw[0, g] = load(adj, g)
-        araw[1, 0] = load(adj, 0, 1)
-        load_chunk(1)
+            a0raw[g] = load(adj, g)
+        first[1] = [load(adj, g, 1) for g in range(2)]
+        w_raw = new([P, 4, HID], BF16, "wraw", 1)
+
+        def load_chunk(c):
+            if c == 1:
+                second[c] = [load(adj, g, c) for g in (2, 3)]
+                nc.sync.dma_start(out=w_raw[:], in_=W_in.rearrange("(p a) h -> p a h", a=4))
+            else:
+                second[c] = load2(adj_rows(2, c), adj_rows(3, c))
+            if c + 1 < NB:
+                first[c + 1] = [load(adj, 0, c + 1)]
+            if 2 <= c < NB - 1:
+                last[c] = load2(adj_rows(NB - 1, c), rows(x, c - 2, slice(0, IN)))
+            else:
+                last[c] = load(adj, NB - 1, c)
+            if c + 1 < NB:
+                first[c + 1].append(load(adj, 1, c + 1))
+            else:
+                for k in range(c - 2, NB):
+                    xraw[k] = load(x, k)
 
         nc.vector.tensor_scalar_add(r[:], r[:], 1.0)
         rec = new([P, NB, 4], F32, "rec", 1)
         nc.vector.reciprocal(out=rec[:], in_=r[:])
 
         def scale_g(g):
-            t = new([P, 4, HID], BF16, "g2", 3)
+            t = new([P, 4, HID], BF16, "d", 3)
             for j in range(4):
                 nc.vector.tensor_scalar_mul(t[:, j, :], graw[g][:, j, :], rec[:, g, j : j + 1])
             return t
 
-        def interleave_g(eng, dst, src, u):
+        def inter_g_half(eng, dst, src, u):
             copy(
                 eng,
                 dst[:, 2 * HID * u : 2 * HID * (u + 1)].rearrange("p (e m j) -> p m j e", e=2, j=4),
                 src[:].rearrange("p j (m u e) -> p u m j e", u=2, e=2)[:, u],
             )
 
-        def interleave_g_all(eng, src):
-            dst = ilv_tile()
+        def inter_g(eng, dst, src):
             copy(
                 eng,
-                dst[:].rearrange("p (t m j) -> p m j t", t=4, j=4),
+                dst.rearrange("p (t m j) -> p m j t", t=4, j=4),
                 src[:].rearrange("p j (m t) -> p m j t", t=4),
             )
-            return dst
 
-        dh = {}
-        gcodes, xcodes, kcodes, acodes, ailv = {}, {}, {}, {}, {}
+        dh, gq, xq, kq, acc = {}, {}, {}, {}, {}
 
-        def inter(eng, c, g, lo=0, hi=B):
-            if (c, g) not in ailv:
-                ailv[c, g] = ilv_tile()
-            interleave(eng, ailv[c, g], araw[c, g], lo, hi)
-
-        def quant_a(c, g):
-            acodes[c, g] = quantize(ailv[c, g], "a", 4, E4)
-
-        def dh_mul(c, g):
-            for t in range(4):
+        def dh_mul(g, a, ts=range(4)):
+            for t in ts:
                 if g == 0:
                     dh[t] = bank("dh" + str(t))
-                mm(dh[t], gcodes[g], slice(P * t, P * (t + 1)), E5, acodes[c, g], E4, g == 0, g == NB - 1)
+                mm(dh[t], gq[g], t, E5, a, E4, g == 0, g == NB - 1)
 
-        def w_flip():
-            w_words = w_raw[:].bitcast(F32)
-            out = []
-            for b in range(2):
-                xt = bank("w" + str(2 + b))[:].rearrange("p (a u i) -> p a u i", a=2, u=2)
-                for a in range(2):
-                    for u in range(2):
-                        nc.tensor.transpose(xt[:, a, u, :], w_words[:, 2 * b + a, u : HID // 2 : 2], ident[:])
-                out.append(xt)
-            return out
+        gall = codes("g", 1, NB)
+        for g in range(NB):
+            gq[g] = part(gall, B * g, B * (g + 1))
 
-        def w_copy(xts):
-            dst = ilv_tile()
-            dv = dst[:].bitcast(F32).rearrange("p (i b a u) -> p b i a u", b=2, a=2, u=2)
-            for b in range(2):
-                nc.scalar.copy(out=dv[:, b], in_=xts[b].rearrange("p a u i -> p i a u"))
-            return dst
+        def head_pass(g, src):
+            dh_mul(g, quant1(src, "one", 4, E4))
 
-        def quant_g(g):
-            gcodes[g] = quantize(gi[g], "g", NB, E5)
-
-        def head_pass(g):
-            quant_a(0, g)
-            dh_mul(0, g)
-
-        gi = {0: ilv_tile()}
-        g2 = scale_g(0)
-        interleave_g("V", gi[0], g2, 0)
-        interleave_g("S", gi[0], g2, 1)
-        gi[1] = interleave_g_all("S", scale_g(1))
-        g2 = scale_g(2)
-        quant_g(0)
-        gi[2] = interleave_g_all("V", g2)
-        inter("S", 0, 0)
-        g2 = scale_g(3)
-        quant_g(1)
-        gi[3] = interleave_g_all("V", g2)
-        inter("S", 0, 1)
-        head_pass(0)
-        g2 = scale_g(4)
-        quant_g(2)
-        head_pass(1)
-        gi[4] = interleave_g_all("V", g2)
-        inter("S", 0, 2)
-        quant_g(3)
-        inter("S", 0, 3)
-        head_pass(2)
-        quant_g(4)
-        inter("S", 0, 4, HEAD, B)
-        inter("V", 0, 4, 0, HEAD)
+        ga, gb, aa = pair(), pair(), pair()
+        s0 = scale_g(0)
+        inter_g_half("V", half(ga, 0), s0, 0)
+        inter_g_half("S", half(ga, 0), s0, 1)
+        inter_g("S", half(ga, 1), scale_g(1))
+        s2 = scale_g(2)
+        quant(gq[0], half(ga, 0), E5)
+        inter_g("V", half(gb, 0), s2)
+        interleave("S", half(aa, 0), a0raw[0], 0, B)
+        s3 = scale_g(3)
+        quant(gq[1], half(ga, 1), E5)
+        inter_g("V", half(gb, 1), s3)
+        interleave("S", half(aa, 1), a0raw[1], 0, B)
+        head_pass(0, half(aa, 0))
+        load_chunk(1)
+        s4 = scale_g(4)
+        quant(part(gall, 2 * B, 4 * B), gb[:], E5)
+        head_pass(1, half(aa, 1))
+        gc, ab = pair(), pair()
+        inter_g("V", half(gc, 0), s4)
+        interleave("S", half(ab, 0), a0raw[2], 0, B)
+        interleave("S", half(ab, 1), a0raw[3], 0, B)
+        head_pass(2, half(ab, 0))
+        quant(gq[4], half(gc, 0), E5)
+        interleave("S", half(gc, 1), a0raw[4], HEAD, B)
+        interleave("V", half(gc, 1), a0raw[4], 0, HEAD)
+        p0 = pair()
+        interleave("S", half(p0, 0), first[1][0], 0, B)
+        head_pass(3, half(ab, 1))
+        head_pass(4, half(gc, 1))
+        interleave("V", half(p0, 1), first[1][1], 0, B)
         load_chunk(2)
-        inter("S", 1, 0)
-        head_pass(3)
-        head_pass(4)
-        inter("V", 1, 1)
-        w_banks = w_flip()
 
-        def evict(engs):
-            d = new([P, 4 * B], BF16, "d", 2)
-            for t in range(4):
-                copy(
-                    engs[t],
-                    d[:, B * t : B * (t + 1)].rearrange("p (u m e) -> p u m e", u=2, e=2),
-                    dh[t][:].rearrange("p (m u e) -> p u m e", u=2, e=2),
-                )
-            return d
-
-        def inter_h(dst, d, u):
-            nc.vector.tensor_copy(
-                out=dst[:, 2 * B * u : 2 * B * (u + 1)].rearrange("p (e m t) -> p m t e", e=2, t=4),
-                in_=d[:].rearrange("p (t u m e) -> p u m t e", t=4, u=2, e=2)[:, u],
-            )
-
-        def inter_h_all(dst, d):
-            nc.vector.tensor_copy(
-                out=dst[:].rearrange("p (u e m t) -> p u m t e", u=2, e=2, t=4),
-                in_=d[:].rearrange("p (t u m e) -> p u m t e", t=4, u=2, e=2),
-            )
-
-        def flip(d, tags):
+        def transposes(tags, block):
             out = []
             for b in range(2):
                 xt = bank(tags[b])[:].rearrange("p (t u m) -> p t u m", t=2, u=2)
                 for t in range(2):
-                    words = d[:, B * (2 * b + t) : B * (2 * b + t + 1)].bitcast(F32)
                     for u in range(2):
-                        nc.tensor.transpose(xt[:, t, u, :], words[:, P * u : P * (u + 1)], ident[:])
+                        nc.tensor.transpose(xt[:, t, u, :], block(2 * b + t, u), ident[:])
                 out.append(xt)
             return out
 
-        def flip_copy(xts, engs):
-            dst = ilv_tile()
-            dv = dst[:].bitcast(F32).rearrange("p (b t m u) -> p b t m u", b=2, t=2, u=2)
-            for b in range(2):
-                copy(engs[b], dv[:, b], xts[b].rearrange("p t u m -> p t m u"))
-            return dst
+        w_words = w_raw[:].bitcast(F32)
+
+        def evict():
+            d = new([P, 4 * B], BF16, "d", 3)
+            for t in range(4):
+                nc.scalar.copy(
+                    out=d[:, B * t : B * (t + 1)].rearrange("p (u m e) -> p u m e", u=2, e=2),
+                    in_=dh[t][:].rearrange("p (m u e) -> p u m e", u=2, e=2),
+                )
+            return d
+
+        def inter_h(dst, d):
+            nc.vector.tensor_copy(
+                out=dst.rearrange("p (u e m t) -> p u m t e", u=2, e=2, t=4),
+                in_=d[:].rearrange("p (t u m e) -> p u m t e", t=4, u=2, e=2),
+            )
+
+        def flip(d, tags):
+            words = d[:].bitcast(F32)
+            return transposes(tags, lambda t, u: words[:, H * t + P * u : H * t + P * (u + 1)])
+
+        def flip_copy(dst, xts, b, eng="S"):
+            dv = dst.bitcast(F32).rearrange("p (b t m u) -> p b t m u", b=2, t=2, u=2)
+            copy(eng, dv[:, b], xts[b].rearrange("p t u m -> p t m u"))
 
         def dx_mul(h, b, tag):
             o = bank(tag)
-            mm(o, h, slice(P * b, P * (b + 1)), E5, wcodes[0], E4, True, True)
+            mm(o, h, b, E5, wq[0], E4, True, True)
             return o
 
-        def dx_store(c, b, o, eng):
-            t = new([P, IN], F32, "out", 12)
+        def dx_store(c, b, o, eng="S"):
+            t = new([P, IN], F32, "out", 8)
             copy(eng, t[:], o[:])
             nc.sync.dma_start(out=rows(out_0, c, slice(0, IN))[:, b, :], in_=t[:])
 
-        acc, wcodes, w_ilv = {}, [], []
-
         def dw_mul(a, c):
             if c == 0:
-                acc[a] = bank("w" + str((a + 2) % 4))
-            mm(acc[a], xcodes[c], slice(P * a, P * (a + 1)), E4, kcodes[c], E5, c == 0, c == NB - 1)
+                acc[a] = bank(("w" if a < 2 else "dh") + str(2 + a % 2))
+            mm(acc[a], xq[c], a, E4, kq[c], E5, c == 0, c == NB - 1)
 
         def dw_store(a, eng):
-            t = new([P, HID], F32, "out", 12)
+            t = new([P, HID], F32, "out", 8)
             copy(
                 eng,
                 t[:].rearrange("p (m t) -> p m t", t=4),
@@ -279,74 +271,91 @@ def tile_allgnn_pa_v_kernel(tc, x, adj, W_in, b_in, deg, grad_out, out_0, out_1)
             )
             nc.sync.dma_start(out=out_1[P * a : P * (a + 1), :], in_=t[:])
 
-        def inter_x(eng, c):
-            t = ilv_tile()
-            interleave(eng, t, xraw[c])
-            return t
+        kh, p1 = pair(), pair()
+        d = evict()
+        dh_mul(0, quant1(half(p0, 0), "one", 4, E4))
+        interleave("V", half(p1, 0), second[1][0], 0, B)
+        xts = flip(d, ["w0", "w1"])
+        dh_mul(1, quant1(half(p0, 1), "one", 4, E4))
+        w_banks = transposes(["w2", "w3"], lambda a, u: w_words[:, a, u : HID // 2 : 2])
+        inter_h(half(kh, 1), d)
+        dh_mul(2, quant1(half(p1, 0), "one", 4, E4))
+        interleave("S", half(p1, 1), second[1][1], 0, B)
+        h = quant1(half(kh, 1), "h", 1, E5)
+        p0, p2 = pair(), pair()
+        interleave("V", half(p2, 0), last[1], 0, B)
+        dv = half(kh, 0).bitcast(F32).rearrange("p (i b a u) -> p b i a u", b=2, a=2, u=2)
+        w_ilv, kh = half(kh, 0), pair()
+        for b in range(2):
+            flip_copy(half(kh, 0), xts, b)
+        for b in range(2):
+            nc.scalar.copy(out=dv[:, b], in_=w_banks[b].rearrange("p a u i -> p i a u"))
+        dh_mul(3, quant1(half(p1, 1), "one", 4, E4))
+        interleave("V", half(p0, 0), first[2][0], 0, B)
+        wq = [quant1(w_ilv, "w", 1, E4)]
+        interleave("S", half(p0, 1), first[2][1], 0, B)
+        o = [dx_mul(h, b, "w" + str(b)) for b in range(2)]
+        dh_mul(4, quant1(half(p2, 0), "one", 4, E4))
+        load_chunk(3)
+        for b in range(2):
+            dx_store(0, b, o[b])
+        late = [dx_mul(h, b + 2, "w" + str(b)) for b in range(2)]
 
-        def front(c):
-            d = evict("SSSS")
-            if c == 1:
-                w_ilv.append(w_copy(w_banks))
-            quant_a(c, 0)
-            dh_mul(c, 0)
+        for c in range(2, NB):
+            d = evict()
+            for b in range(2):
+                dx_store(c - 2, b + 2, late[b])
+            p1 = pair()
+            a = quant2(p0, "two", 2, E4)
+            interleave("V", p1[:], second[c], 0, 2 * B)
+            dh_mul(0, a[0])
+            dh_mul(1, a[1])
             xts = flip(d, ["w0", "w1"])
-            inter("V", c, 2)
-            quant_a(c, 1)
-            dh_mul(c, 1)
-            inter("S", c, 3)
-            hi = ilv_tile()
-            inter_h_all(hi, d)
-            quant_a(c, 2)
-            kn = flip_copy(xts, "SS")
-            dh_mul(c, 2)
-            return quantize(hi, "h", 2, E5), kn
-
-        for c in range(1, NB - 1):
-            h, kn = front(c)
-            if c == 1:
-                wcodes.append(quantize(w_ilv[0], "wq", 1, E4))
-            inter("V", c, 4)
+            inter_h(half(kh, 1), d)
+            a = quant2(p1, "two", 2, E4)
+            dh_mul(2, a[0])
+            dh_mul(3, a[1])
+            if c == NB - 1:
+                break
+            p0, p2 = pair(), pair()
+            interleave("S", half(p0, 0), first[c + 1][0], 0, B)
+            interleave("V", p2[:], last[c], 0, 2 * B)
+            kq[c - 2], h = quant2(kh, "kh", 3, E5)
+            kh = pair()
+            for b in range(2):
+                flip_copy(half(kh, 0), xts, b)
+            interleave("S", half(p0, 1), first[c + 1][1], 0, B)
             o = [dx_mul(h, b, "w" + str(b)) for b in range(2)]
+            a4, xq[c - 2] = quant2(p2, "ax", 2, E4)
+            dh_mul(4, a4)
             if c + 2 < NB:
                 load_chunk(c + 2)
-            inter("S", c + 1, 0, 0, FIRST)
-            quant_a(c, 3)
-            quant_a(c, 4)
-            xi = inter_x("V", c - 1)
             for b in range(2):
-                dx_store(c - 1, b, o[b], "S")
-            dh_mul(c, 3)
-            o = [dx_mul(h, b + 2, "w" + str(b)) for b in range(2)]
-            dh_mul(c, 4)
-            inter("S", c + 1, 0, FIRST, B)
-            kcodes[c - 1] = quantize(kn, "k", NB, E5)
-            xcodes[c - 1] = quantize(xi, "x", NB, E4)
-            dw_mul(0, c - 1)
-            dw_mul(1, c - 1)
-            for b in range(2):
-                dx_store(c - 1, b + 2, o[b], "S")
-            inter("V", c + 1, 1)
+                dx_store(c - 1, b, o[b])
+            late = [dx_mul(h, b + 2, "w" + str(b)) for b in range(2)]
+            dw_mul(0, c - 2)
+            dw_mul(1, c - 2)
 
         c = NB - 1
-        H = B // 2
-        h, kn = front(c)
-        o = [dx_mul(h, b, "w" + str(b)) for b in range(2)]
-        quant_a(c, 3)
-        inter("S", c, 4, LAST, B)
-        inter("V", c, 4, 0, LAST)
+        p2 = pair()
+        interleave("S", half(p2, 0), last[c], 0, B)
+        kq[c - 2], h = quant2(kh, "kh", 3, E5)
+        kh = pair()
         for b in range(2):
-            dx_store(c - 1, b, o[b], "S")
-        dh_mul(c, 3)
-        kcodes[c - 1] = quantize(kn, "k", NB, E5)
-        quant_a(c, 4)
-        o2 = dx_mul(h, 2, "w0")
-        dh_mul(c, 4)
-        o3 = dx_mul(h, 3, "w1")
-        dx_store(c - 1, 2, o2, "S")
-        xi = ilv_tile()
-        interleave("V", xi, xraw[c - 1], 0, XV)
-        d = new([P, 4 * B], BF16, "d", 2)
+            flip_copy(half(kh, 0), xts, b)
+        o = [dx_mul(h, b, "w" + str(b)) for b in range(2)]
+        a4 = quant1(half(p2, 0), "one", 4, E4)
+        dh_mul(4, a4)
+        interleave("S", half(p2, 1), xraw[c - 2], 0, X2S)
+        interleave("V", half(p2, 1), xraw[c - 2], X2S, B)
+        for b in range(2):
+            dx_store(c - 1, b, o[b])
+        late = [dx_mul(h, b + 2, "w" + str(b)) for b in range(2)]
+        xx = pair()
+        interleave("V", half(xx, 0), xraw[c - 1], 0, B)
+
+        xq[c - 2] = quant1(half(p2, 1), "x2", 1, E4)
+        d = new([P, 4 * B], BF16, "d", 3)
 
         def evict_half(u, engs):
             for t in range(4):
@@ -356,58 +365,59 @@ def tile_allgnn_pa_v_kernel(tc, x, adj, W_in, b_in, deg, grad_out, out_0, out_1)
                     dh[t][:].rearrange("p (m u e) -> p u m e", u=2, e=2)[:, u],
                 )
 
-        hi = ilv_tile()
-        hc, hs = codes("h", 2)
+        def inter_h_half(dst, u):
+            nc.vector.tensor_copy(
+                out=dst[:, 2 * B * u : 2 * B * (u + 1)].rearrange("p (e m t) -> p m t e", e=2, t=4),
+                in_=d[:].rearrange("p (t u m e) -> p u m t e", t=4, u=2, e=2)[:, u],
+            )
+
+        hq = part(codes("one", 4, 1), 0, B)
+        hi = half(kh, 1)
 
         def dx_half(u):
-            cols = slice(H * u, H * (u + 1))
-            nc.vector.quantize_mx(out=hc[:, cols].bitcast(E5), scales=hs[:, cols], in_=hi[:, 4 * H * u : 4 * H * (u + 1)])
-            return [dx_mul((hc, hs), b, "dh" + str((b + 2) % 4)) for b in (2 * u, 2 * u + 1)]
+            quant(part(hq, H * u, H * (u + 1)), hi[:, 4 * H * u : 4 * H * (u + 1)], E5)
+            return [dx_mul(hq, b, ("w", "dh")[u] + str(b % 2)) for b in (2 * u, 2 * u + 1)]
 
-        xl = ilv_tile()
-        xcodes[c] = codes("x", NB)
-
-        def x_part(eng, a):
-            interleave(eng, xl, xraw[c], P * a, P * (a + 1))
-
-        def dw_last(a):
-            xc, xs = xcodes[c]
-            cols = slice(P * a, P * (a + 1))
-            nc.vector.quantize_mx(out=xc[:, cols].bitcast(E4), scales=xs[:, cols], in_=xl[:, B * a : B * (a + 1)])
-            dw_mul(a, c)
-
+        dw_mul(0, c - 2)
+        dw_mul(1, c - 2)
         evict_half(0, "SVSV")
         evict_half(1, "SSSS")
-        interleave("V", xi, xraw[c - 1], XV, B)
-        inter_h(hi, d, 0)
-        dx_store(c - 1, 3, o3, "S")
-        for k in range(NB - 2):
-            dw_mul(2, k)
-        xts = flip(d, ["dh0", "dh1"])
-        kn = flip_copy(xts, "SS")
-        dw_mul(3, 0)
-        x_part("V", 0)
-        o = dx_half(0)
-        inter_h(hi, d, 1)
-        xcodes[c - 1] = quantize(xi, "x", NB, E4)
-        for k in range(1, NB - 2):
-            dw_mul(3, k)
-        dw_mul(0, c - 1)
-        o.extend(dx_half(1))
+        kq[c - 1] = quant1(half(kh, 0), "one", 4, E5)
+        inter_h_half(hi, 0)
+        xq[c - 1] = quant1(half(xx, 0), "one", 4, E4)
         for b in range(2):
-            dx_store(c, b, o[b], "S")
-        kcodes[c] = quantize(kn, "k", NB, E5)
+            dx_store(c - 1, b + 2, late[b])
+        xts = flip(d, ["dh0", "dh1"])
+        kl = pair()
+        flip_copy(half(kl, 0), xts, 0)
+        dw_mul(2, 0)
+        dw_mul(2, 1)
+        o = dx_half(0)
+        inter_h_half(hi, 1)
+        flip_copy(half(kl, 0), xts, 1, "V")
+        dw_mul(2, 2)
+        dw_mul(0, c - 1)
         dw_mul(1, c - 1)
-        dw_last(0)
-        x_part("V", 1)
-        x_part("S", 3)
-        dx_store(c, 2, o[2], "S")
-        x_part("V", 2)
-        for a in range(2, 4):
+        o.extend(dx_half(1))
+        for b in range(4):
+            dx_store(c, b, o[b])
+        xl = half(xx, 1)
+        xq[c] = part(codes("xl", 1, 1), 0, B)
+
+        def x_last(u):
+            quant(part(xq[c], H * u, H * (u + 1)), xl[:, 4 * H * u : 4 * H * (u + 1)], E4)
+
+        interleave("V", xl, xraw[c], 0, H)
+        kq[c] = quant1(half(kl, 0), "kl", 1, E5)
+        x_last(0)
+        interleave("V", xl, xraw[c], H, B)
+        for k in range(NB - 2):
+            dw_mul(3, k)
+        dw_mul(0, c)
+        dw_mul(1, c)
+        x_last(1)
+        for a in (2, 3):
             dw_mul(a, c - 1)
-        for a in range(1, 4):
-            dw_last(a)
-        dx_store(c, 3, o[3], "S")
-        dw_store(0, "V")
-        for a in range(1, 4):
-            dw_store(a, "SV"[(a + 1) % 2])
+            dw_mul(a, c)
+        for a in range(4):
+            dw_store(a, "SV"[a % 2])

@@ -21,8 +21,11 @@ B = 512
 NB = N // B
 H = B // 2
 RUN = 8
-HEAD = 384
+HEAD = 128
 X2S = 320
+LAG = 2
+GV = 40
+AV = 256
 
 
 def tile_allgnn_pa_v_kernel(tc, x, adj, W_in, b_in, deg, grad_out, out_0, out_1):
@@ -114,11 +117,16 @@ def tile_allgnn_pa_v_kernel(tc, x, adj, W_in, b_in, deg, grad_out, out_0, out_1)
         graw[0] = new([P, 4, B], BF16, "raw", 12)
         for j in (0, 2):
             nc.sync.dma_start(out=graw[0][:, j : j + 2, :], in_=rows(grad_out, 0, slice(0, HID))[:, j : j + 2, :])
-        graw[1] = load(grad_out, 1)
+        head = [("g", 0), ("g", 1)]
         for g in range(NB):
             if g + 2 < NB:
-                graw[g + 2] = load(grad_out, g + 2)
-            a0raw[g] = load(adj, g)
+                head.append(("g", g + 2))
+            head.append(("a", g))
+        for kind, g in head[1:]:
+            if kind == "g":
+                graw[g] = load(grad_out, g)
+            else:
+                a0raw[g] = load(adj, g)
         first[1] = [load(adj, g, 1) for g in range(2)]
         w_raw = new([P, 4, HID], BF16, "wraw", 1)
 
@@ -128,11 +136,13 @@ def tile_allgnn_pa_v_kernel(tc, x, adj, W_in, b_in, deg, grad_out, out_0, out_1)
                 nc.sync.dma_start(out=w_raw[:], in_=W_in.rearrange("(p a) h -> p a h", a=4))
             else:
                 second[c] = load2(adj_rows(2, c), adj_rows(3, c))
+            if c == 1:
+                last[c] = load(adj, NB - 1, c)
             if c + 1 < NB:
                 first[c + 1] = [load(adj, 0, c + 1)]
             if 2 <= c < NB - 1:
                 last[c] = load2(adj_rows(NB - 1, c), rows(x, c - 2, slice(0, IN)))
-            else:
+            elif c > 1:
                 last[c] = load(adj, NB - 1, c)
             if c + 1 < NB:
                 first[c + 1].append(load(adj, 1, c + 1))
@@ -150,19 +160,15 @@ def tile_allgnn_pa_v_kernel(tc, x, adj, W_in, b_in, deg, grad_out, out_0, out_1)
                 nc.vector.tensor_scalar_mul(t[:, j, :], graw[g][:, j, :], rec[:, g, j : j + 1])
             return t
 
-        def inter_g_half(eng, dst, src, u):
-            copy(
-                eng,
-                dst[:, 2 * HID * u : 2 * HID * (u + 1)].rearrange("p (e m j) -> p m j e", e=2, j=4),
-                src[:].rearrange("p j (m u e) -> p u m j e", u=2, e=2)[:, u],
-            )
+        def inter_g(dst, src):
+            dv = dst.rearrange("p (t m j) -> p m j t", t=4, j=4)
+            sv = src[:].rearrange("p j (m t) -> p m j t", t=4)
+            nc.scalar.copy(out=dv[:, GV:], in_=sv[:, GV:])
+            nc.vector.tensor_copy(out=dv[:, :GV], in_=sv[:, :GV])
 
-        def inter_g(eng, dst, src):
-            copy(
-                eng,
-                dst.rearrange("p (t m j) -> p m j t", t=4, j=4),
-                src[:].rearrange("p j (m t) -> p m j t", t=4),
-            )
+        def shared(dst, src, cut):
+            interleave("S", dst, src, cut, B)
+            interleave("V", dst, src, 0, cut)
 
         dh, gq, xq, kq, acc = {}, {}, {}, {}, {}
 
@@ -176,39 +182,34 @@ def tile_allgnn_pa_v_kernel(tc, x, adj, W_in, b_in, deg, grad_out, out_0, out_1)
         for g in range(NB):
             gq[g] = part(gall, B * g, B * (g + 1))
 
-        def head_pass(g, src):
-            dh_mul(g, quant1(src, "one", 4, E4))
+        tiles = []
 
-        ga, gb, aa = pair(), pair(), pair()
-        s0 = scale_g(0)
-        inter_g_half("V", half(ga, 0), s0, 0)
-        inter_g_half("S", half(ga, 0), s0, 1)
-        inter_g("S", half(ga, 1), scale_g(1))
-        s2 = scale_g(2)
-        quant(gq[0], half(ga, 0), E5)
-        inter_g("V", half(gb, 0), s2)
-        interleave("S", half(aa, 0), a0raw[0], 0, B)
-        s3 = scale_g(3)
-        quant(gq[1], half(ga, 1), E5)
-        inter_g("V", half(gb, 1), s3)
-        interleave("S", half(aa, 1), a0raw[1], 0, B)
-        head_pass(0, half(aa, 0))
-        load_chunk(1)
-        s4 = scale_g(4)
-        quant(part(gall, 2 * B, 4 * B), gb[:], E5)
-        head_pass(1, half(aa, 1))
-        gc, ab = pair(), pair()
-        inter_g("V", half(gc, 0), s4)
-        interleave("S", half(ab, 0), a0raw[2], 0, B)
-        interleave("S", half(ab, 1), a0raw[3], 0, B)
-        head_pass(2, half(ab, 0))
-        quant(gq[4], half(gc, 0), E5)
-        interleave("S", half(gc, 1), a0raw[4], HEAD, B)
-        interleave("V", half(gc, 1), a0raw[4], 0, HEAD)
+        def finish(i):
+            kind, g = head[i]
+            if kind == "g":
+                quant(gq[g], tiles[i], E5)
+            else:
+                dh_mul(g, quant1(tiles[i], "one", 4, E4))
+
+        for i, (kind, g) in enumerate(head):
+            if i % 2 == 0:
+                t = pair()
+                tiles.extend([half(t, 0), half(t, 1)])
+            if kind == "g":
+                s = scale_g(g)
+            if i >= LAG:
+                finish(i - LAG)
+            if kind == "g":
+                inter_g(tiles[i], s)
+            else:
+                shared(tiles[i], a0raw[g], AV)
+            if i == NB:
+                load_chunk(1)
+        for i in range(len(head) - LAG, len(head) - 1):
+            finish(i)
         p0 = pair()
-        interleave("S", half(p0, 0), first[1][0], 0, B)
-        head_pass(3, half(ab, 1))
-        head_pass(4, half(gc, 1))
+        shared(half(p0, 0), first[1][0], HEAD)
+        finish(len(head) - 1)
         interleave("V", half(p0, 1), first[1][1], 0, B)
         load_chunk(2)
 
@@ -291,24 +292,28 @@ def tile_allgnn_pa_v_kernel(tc, x, adj, W_in, b_in, deg, grad_out, out_0, out_1)
         for b in range(2):
             nc.scalar.copy(out=dv[:, b], in_=w_banks[b].rearrange("p a u i -> p i a u"))
         dh_mul(3, quant1(half(p1, 1), "one", 4, E4))
-        interleave("V", half(p0, 0), first[2][0], 0, B)
-        wq = [quant1(w_ilv, "w", 1, E4)]
-        interleave("S", half(p0, 1), first[2][1], 0, B)
-        o = [dx_mul(h, b, "w" + str(b)) for b in range(2)]
         dh_mul(4, quant1(half(p2, 0), "one", 4, E4))
+        wq = [quant1(w_ilv, "w", 1, E4)]
+        interleave("S", half(p0, 0), first[2][0], 0, B)
+        interleave("V", half(p0, 1), first[2][1], 0, B)
+        early = [dx_mul(h, b, "w" + str(b)) for b in range(2)]
         load_chunk(3)
-        for b in range(2):
-            dx_store(0, b, o[b])
-        late = [dx_mul(h, b + 2, "w" + str(b)) for b in range(2)]
 
         for c in range(2, NB):
             d = evict()
+            if c == 2:
+                a = [quant1(half(p0, i), "one", 4, E4) for i in range(2)]
+                dh_mul(0, a[0])
+                for b in range(2):
+                    dx_store(0, b, early[b])
+                late = [dx_mul(h, b + 2, "w" + str(b)) for b in range(2)]
+            else:
+                a = quant2(p0, "two", 2, E4)
+                dh_mul(0, a[0])
             for b in range(2):
                 dx_store(c - 2, b + 2, late[b])
             p1 = pair()
-            a = quant2(p0, "two", 2, E4)
             interleave("V", p1[:], second[c], 0, 2 * B)
-            dh_mul(0, a[0])
             dh_mul(1, a[1])
             xts = flip(d, ["w0", "w1"])
             inter_h(half(kh, 1), d)

@@ -95,18 +95,9 @@ def tile_allgnn_pa_v_kernel(tc, x, adj, W_in, b_in, deg, grad_out, out_0, out_1)
             )
 
         def load(ap, g, c=0):
-            t = new([P, 4, B], BF16, "raw", 12)
+            t = new([P, 4, B], BF16, "raw", 15)
             nc.sync.dma_start(out=t[:], in_=rows(ap, g, slice(B * c, B * (c + 1))))
             return t
-
-        def load2(a, b):
-            t = new([P, 4, 2 * B], BF16, "raw2", 4)
-            nc.sync.dma_start(out=t[:, :, :B], in_=a)
-            nc.sync.dma_start(out=t[:, :, B:], in_=b)
-            return t
-
-        def adj_rows(g, c):
-            return rows(adj, g, slice(B * c, B * (c + 1)))
 
         r = new([P, NB, 4], F32, "deg", 1)
         nc.sync.dma_start(out=r[:], in_=deg.rearrange("(g p j) -> p g j", p=P, j=4))
@@ -114,7 +105,7 @@ def tile_allgnn_pa_v_kernel(tc, x, adj, W_in, b_in, deg, grad_out, out_0, out_1)
         make_identity(nc, ident[:])
 
         graw, a0raw, first, second, last, xraw = {}, {}, {}, {}, {}, {}
-        graw[0] = new([P, 4, B], BF16, "raw", 12)
+        graw[0] = new([P, 4, B], BF16, "raw", 15)
         for j in (0, 2):
             nc.sync.dma_start(out=graw[0][:, j : j + 2, :], in_=rows(grad_out, 0, slice(0, HID))[:, j : j + 2, :])
         head = [("g", 0), ("g", 1)]
@@ -131,23 +122,19 @@ def tile_allgnn_pa_v_kernel(tc, x, adj, W_in, b_in, deg, grad_out, out_0, out_1)
         w_raw = new([P, 4, HID], BF16, "wraw", 1)
 
         def load_chunk(c):
+            second[c] = [load(adj, g, c) for g in (2, 3)]
             if c == 1:
-                second[c] = [load(adj, g, c) for g in (2, 3)]
                 nc.sync.dma_start(out=w_raw[:], in_=W_in.rearrange("(p a) h -> p a h", a=4))
-            else:
-                second[c] = load2(adj_rows(2, c), adj_rows(3, c))
-            if c == 1:
                 last[c] = load(adj, NB - 1, c)
             if c + 1 < NB:
                 first[c + 1] = [load(adj, 0, c + 1)]
-            if 2 <= c < NB - 1:
-                last[c] = load2(adj_rows(NB - 1, c), rows(x, c - 2, slice(0, IN)))
-            elif c > 1:
+            if c >= 2:
                 last[c] = load(adj, NB - 1, c)
+                xraw[c - 2] = load(x, c - 2)
             if c + 1 < NB:
                 first[c + 1].append(load(adj, 1, c + 1))
             else:
-                for k in range(c - 2, NB):
+                for k in range(c - 1, NB):
                     xraw[k] = load(x, k)
 
         nc.vector.tensor_scalar_add(r[:], r[:], 1.0)
@@ -253,10 +240,27 @@ def tile_allgnn_pa_v_kernel(tc, x, adj, W_in, b_in, deg, grad_out, out_0, out_1)
             mm(o, h, b, E5, wq[0], E4, True, True)
             return o
 
-        def dx_store(c, b, o, eng="S"):
-            t = new([P, IN], F32, "out", 8)
-            copy(eng, t[:], o[:])
-            nc.sync.dma_start(out=rows(out_0, c, slice(0, IN))[:, b, :], in_=t[:])
+        waiting, stage = [], []
+
+        def out_half(i):
+            if i % 2 == 0:
+                stage.append(new([P, 2, IN], F32, "out", 10))
+            return stage[-1][:, i % 2, :]
+
+        def flush():
+            for dst, src in waiting:
+                nc.sync.dma_start(out=dst, in_=src)
+            waiting.clear()
+
+        def dx_store(c, b, o):
+            t = out_half(b)
+            nc.scalar.copy(out=t, in_=o[:])
+            if c == NB - 1:
+                nc.sync.dma_start(out=rows(out_0, c, slice(0, IN))[:, b, :], in_=t)
+            elif b % 2 == 1:
+                waiting.append((rows(out_0, c, slice(0, IN))[:, b - 1 : b + 1, :], stage[-1][:]))
+                if c > 0:
+                    flush()
 
         def dw_mul(a, c):
             if c == 0:
@@ -264,13 +268,13 @@ def tile_allgnn_pa_v_kernel(tc, x, adj, W_in, b_in, deg, grad_out, out_0, out_1)
             mm(acc[a], xq[c], a, E4, kq[c], E5, c == 0, c == NB - 1)
 
         def dw_store(a, eng):
-            t = new([P, HID], F32, "out", 8)
+            t = out_half(a)
             copy(
                 eng,
-                t[:].rearrange("p (m t) -> p m t", t=4),
+                t.rearrange("p (m t) -> p m t", t=4),
                 acc[a][:].rearrange("p (t m) -> p m t", t=4),
             )
-            nc.sync.dma_start(out=out_1[P * a : P * (a + 1), :], in_=t[:])
+            nc.sync.dma_start(out=out_1[P * a : P * (a + 1), :], in_=t)
 
         kh, p1 = pair(), pair()
         d = evict()
@@ -313,7 +317,8 @@ def tile_allgnn_pa_v_kernel(tc, x, adj, W_in, b_in, deg, grad_out, out_0, out_1)
             for b in range(2):
                 dx_store(c - 2, b + 2, late[b])
             p1 = pair()
-            interleave("V", p1[:], second[c], 0, 2 * B)
+            for i in range(2):
+                interleave("V", half(p1, i), second[c][i], 0, B)
             dh_mul(1, a[1])
             xts = flip(d, ["w0", "w1"])
             inter_h(half(kh, 1), d)
@@ -324,7 +329,8 @@ def tile_allgnn_pa_v_kernel(tc, x, adj, W_in, b_in, deg, grad_out, out_0, out_1)
                 break
             p0, p2 = pair(), pair()
             interleave("S", half(p0, 0), first[c + 1][0], 0, B)
-            interleave("V", p2[:], last[c], 0, 2 * B)
+            interleave("V", half(p2, 0), last[c], 0, B)
+            interleave("V", half(p2, 1), xraw[c - 2], 0, B)
             kq[c - 2], h = quant2(kh, "kh", 3, E5)
             kh = pair()
             for b in range(2):

@@ -23,6 +23,7 @@ H = B // 2
 RUN = 8
 HEAD = 128
 X2S = 320
+MID = 448
 LAG = 2
 GV = 40
 AV = 256
@@ -125,11 +126,10 @@ def tile_allgnn_pa_v_kernel(tc, x, adj, W_in, b_in, deg, grad_out, out_0, out_1)
             second[c] = [load(adj, g, c) for g in (2, 3)]
             if c == 1:
                 nc.sync.dma_start(out=w_raw[:], in_=W_in.rearrange("(p a) h -> p a h", a=4))
-                last[c] = load(adj, NB - 1, c)
+            last[c] = load(adj, NB - 1, c)
             if c + 1 < NB:
                 first[c + 1] = [load(adj, 0, c + 1)]
             if c >= 2:
-                last[c] = load(adj, NB - 1, c)
                 xraw[c - 2] = load(x, c - 2)
             if c + 1 < NB:
                 first[c + 1].append(load(adj, 1, c + 1))
@@ -148,8 +148,8 @@ def tile_allgnn_pa_v_kernel(tc, x, adj, W_in, b_in, deg, grad_out, out_0, out_1)
             return t
 
         def inter_g(dst, src):
-            dv = dst.rearrange("p (t m j) -> p m j t", t=4, j=4)
-            sv = src[:].rearrange("p j (m t) -> p m j t", t=4)
+            dv = dst.rearrange("p (t m u e) -> p m u t e", t=4, u=2, e=2)
+            sv = src[:].rearrange("p (u e) (m t) -> p m u t e", u=2, t=4)
             nc.scalar.copy(out=dv[:, GV:], in_=sv[:, GV:])
             nc.vector.tensor_copy(out=dv[:, :GV], in_=sv[:, :GV])
 
@@ -223,8 +223,8 @@ def tile_allgnn_pa_v_kernel(tc, x, adj, W_in, b_in, deg, grad_out, out_0, out_1)
 
         def inter_h(dst, d):
             nc.vector.tensor_copy(
-                out=dst.rearrange("p (u e m t) -> p u m t e", u=2, e=2, t=4),
-                in_=d[:].rearrange("p (t u m e) -> p u m t e", t=4, u=2, e=2),
+                out=dst.rearrange("p (e w s t) -> p w s e t", e=2, s=2, t=2),
+                in_=d[:].rearrange("p (s t w e) -> p w s e t", s=2, t=2, e=2),
             )
 
         def flip(d, tags):
@@ -235,9 +235,9 @@ def tile_allgnn_pa_v_kernel(tc, x, adj, W_in, b_in, deg, grad_out, out_0, out_1)
             dv = dst.bitcast(F32).rearrange("p (b t m u) -> p b t m u", b=2, t=2, u=2)
             copy(eng, dv[:, b], xts[b].rearrange("p t u m -> p t m u"))
 
-        def dx_mul(h, b, tag):
+        def dx_mul(h, b, tag, whole=True):
             o = bank(tag)
-            mm(o, h, b, E5, wq[0], E4, True, True)
+            mm(o, h, 2 * (b % 2) + b // 2 if whole else b, E5, wq[0], E4, True, True)
             return o
 
         waiting, stage = [], []
@@ -316,26 +316,29 @@ def tile_allgnn_pa_v_kernel(tc, x, adj, W_in, b_in, deg, grad_out, out_0, out_1)
                 dh_mul(0, a[0])
             for b in range(2):
                 dx_store(c - 2, b + 2, late[b])
-            p1 = pair()
-            for i in range(2):
-                interleave("V", half(p1, i), second[c][i], 0, B)
+            if c == 2:
+                p1 = pair()
+            interleave("V", half(p1, 0), second[c][0], 0, B if c == 2 else MID)
+            interleave("V", half(p1, 1), second[c][1], 0, B)
             dh_mul(1, a[1])
             xts = flip(d, ["w0", "w1"])
-            inter_h(half(kh, 1), d)
-            a = quant2(p1, "two", 2, E4)
-            dh_mul(2, a[0])
-            dh_mul(3, a[1])
             if c == NB - 1:
                 break
             p0, p2 = pair(), pair()
-            interleave("S", half(p0, 0), first[c + 1][0], 0, B)
             interleave("V", half(p2, 0), last[c], 0, B)
+            a = quant2(p1, "two", 2, E4)
+            dh_mul(2, a[0])
+            dh_mul(3, a[1])
+            inter_h(half(kh, 1), d)
+            interleave("S", half(p0, 0), first[c + 1][0], 0, B)
             interleave("V", half(p2, 1), xraw[c - 2], 0, B)
             kq[c - 2], h = quant2(kh, "kh", 3, E5)
             kh = pair()
             for b in range(2):
                 flip_copy(half(kh, 0), xts, b)
             interleave("S", half(p0, 1), first[c + 1][1], 0, B)
+            p1 = pair()
+            interleave("S", half(p1, 0), second[c + 1][0], MID, B)
             o = [dx_mul(h, b, "w" + str(b)) for b in range(2)]
             a4, xq[c - 2] = quant2(p2, "ax", 2, E4)
             dh_mul(4, a4)
@@ -348,22 +351,25 @@ def tile_allgnn_pa_v_kernel(tc, x, adj, W_in, b_in, deg, grad_out, out_0, out_1)
             dw_mul(1, c - 2)
 
         c = NB - 1
-        p2 = pair()
+        p2, xx = pair(), pair()
         interleave("S", half(p2, 0), last[c], 0, B)
+        interleave("V", half(p2, 1), xraw[c - 2], X2S, B)
+        a = quant2(p1, "two", 2, E4)
+        dh_mul(2, a[0])
+        dh_mul(3, a[1])
+        inter_h(half(kh, 1), d)
+        interleave("V", half(xx, 0), xraw[c - 1], 0, H)
         kq[c - 2], h = quant2(kh, "kh", 3, E5)
         kh = pair()
         for b in range(2):
             flip_copy(half(kh, 0), xts, b)
         o = [dx_mul(h, b, "w" + str(b)) for b in range(2)]
-        a4 = quant1(half(p2, 0), "one", 4, E4)
-        dh_mul(4, a4)
+        dh_mul(4, quant1(half(p2, 0), "one", 4, E4))
         interleave("S", half(p2, 1), xraw[c - 2], 0, X2S)
-        interleave("V", half(p2, 1), xraw[c - 2], X2S, B)
+        interleave("V", half(xx, 0), xraw[c - 1], H, B)
         for b in range(2):
             dx_store(c - 1, b, o[b])
         late = [dx_mul(h, b + 2, "w" + str(b)) for b in range(2)]
-        xx = pair()
-        interleave("V", half(xx, 0), xraw[c - 1], 0, B)
 
         xq[c - 2] = quant1(half(p2, 1), "x2", 1, E4)
         d = new([P, 4 * B], BF16, "d", 3)
@@ -387,7 +393,7 @@ def tile_allgnn_pa_v_kernel(tc, x, adj, W_in, b_in, deg, grad_out, out_0, out_1)
 
         def dx_half(u):
             quant(part(hq, H * u, H * (u + 1)), hi[:, 4 * H * u : 4 * H * (u + 1)], E5)
-            return [dx_mul(hq, b, ("w", "dh")[u] + str(b % 2)) for b in (2 * u, 2 * u + 1)]
+            return [dx_mul(hq, b, ("w", "dh")[u] + str(b % 2), False) for b in (2 * u, 2 * u + 1)]
 
         dw_mul(0, c - 2)
         dw_mul(1, c - 2)

@@ -23,6 +23,8 @@ H = B // 2
 RUN = 8
 HEAD = 128
 X2S = 320
+ONE = 96
+TWO = 416
 MID = 448
 LAG = 2
 GV = 40
@@ -89,11 +91,16 @@ def tile_allgnn_pa_v_kernel(tc, x, adj, W_in, b_in, deg, grad_out, out_0, out_1)
             return t[:, 4 * B * i : 4 * B * (i + 1)]
 
         def interleave(eng, dst, src, lo, hi):
-            copy(
-                eng,
-                dst[:, 4 * lo : 4 * hi].rearrange("p (w i u e) -> p w u i e", i=RUN, u=2, e=2),
-                src[:, :, lo:hi].rearrange("p (u e) (w i) -> p w u i e", i=RUN, u=2),
-            )
+            if eng == "S":
+                nc.scalar.copy(
+                    out=dst[:, 4 * lo : 4 * hi].rearrange("p (w i u e) -> p w u i e", i=RUN, u=2, e=2),
+                    in_=src[:, :, lo:hi].rearrange("p (u e) (w i) -> p w u i e", i=RUN, u=2),
+                )
+            else:
+                nc.vector.tensor_copy(
+                    out=dst[:, 4 * lo : 4 * hi].rearrange("p (w h i j) -> p h w j i", h=2, i=RUN, j=4),
+                    in_=src[:, :, lo:hi].rearrange("p j (w h i) -> p h w j i", h=2, i=RUN),
+                )
 
         def load(ap, g, c=0):
             t = new([P, 4, B], BF16, "raw", 15)
@@ -283,12 +290,12 @@ def tile_allgnn_pa_v_kernel(tc, x, adj, W_in, b_in, deg, grad_out, out_0, out_1)
         xts = flip(d, ["w0", "w1"])
         dh_mul(1, quant1(half(p0, 1), "one", 4, E4))
         w_banks = transposes(["w2", "w3"], lambda a, u: w_words[:, a, u : HID // 2 : 2])
-        inter_h(half(kh, 1), d)
         dh_mul(2, quant1(half(p1, 0), "one", 4, E4))
+        inter_h(half(kh, 1), d)
         interleave("S", half(p1, 1), second[1][1], 0, B)
-        h = quant1(half(kh, 1), "h", 1, E5)
         p0, p2 = pair(), pair()
         interleave("V", half(p2, 0), last[1], 0, B)
+        h = quant1(half(kh, 1), "h", 1, E5)
         dv = half(kh, 0).bitcast(F32).rearrange("p (i b a u) -> p b i a u", b=2, a=2, u=2)
         w_ilv, kh = half(kh, 0), pair()
         for b in range(2):
@@ -298,7 +305,7 @@ def tile_allgnn_pa_v_kernel(tc, x, adj, W_in, b_in, deg, grad_out, out_0, out_1)
         dh_mul(3, quant1(half(p1, 1), "one", 4, E4))
         dh_mul(4, quant1(half(p2, 0), "one", 4, E4))
         wq = [quant1(w_ilv, "w", 1, E4)]
-        interleave("S", half(p0, 0), first[2][0], 0, B)
+        shared(half(p0, 0), first[2][0], ONE)
         interleave("V", half(p0, 1), first[2][1], 0, B)
         early = [dx_mul(h, b, "w" + str(b)) for b in range(2)]
         load_chunk(3)
@@ -311,15 +318,15 @@ def tile_allgnn_pa_v_kernel(tc, x, adj, W_in, b_in, deg, grad_out, out_0, out_1)
                 for b in range(2):
                     dx_store(0, b, early[b])
                 late = [dx_mul(h, b + 2, "w" + str(b)) for b in range(2)]
+                p1 = pair()
+                interleave("S", half(p1, 1), second[c][1], TWO, B)
             else:
                 a = quant2(p0, "two", 2, E4)
                 dh_mul(0, a[0])
             for b in range(2):
                 dx_store(c - 2, b + 2, late[b])
-            if c == 2:
-                p1 = pair()
             interleave("V", half(p1, 0), second[c][0], 0, B if c == 2 else MID)
-            interleave("V", half(p1, 1), second[c][1], 0, B)
+            interleave("V", half(p1, 1), second[c][1], 0, TWO if c == 2 else B)
             dh_mul(1, a[1])
             xts = flip(d, ["w0", "w1"])
             if c == NB - 1:

@@ -93,8 +93,8 @@ def tile_allgnn_pa_v_kernel(tc, x, adj, W_in, b_in, deg, grad_out, out_0, out_1)
         def interleave(eng, dst, src, lo, hi):
             if eng == "S":
                 nc.scalar.copy(
-                    out=dst[:, 4 * lo : 4 * hi].rearrange("p (w i u e) -> p w u i e", i=RUN, u=2, e=2),
-                    in_=src[:, :, lo:hi].rearrange("p (u e) (w i) -> p w u i e", i=RUN, u=2),
+                    out=dst[:, 4 * lo : 4 * hi].rearrange("p (w i j) -> p w j i", i=RUN, j=4),
+                    in_=src[:, :, lo:hi].rearrange("p j (w i) -> p w j i", i=RUN),
                 )
             else:
                 nc.vector.tensor_copy(

@@ -22,10 +22,11 @@ NB = N // B
 H = B // 2
 RUN = 8
 HEAD = 128
-X2S = 320
 ONE = 96
 TWO = 416
-MID = 448
+MID = 288
+CUT = 384
+LAST = 160
 LAG = 2
 GV = 40
 AV = 256
@@ -166,11 +167,42 @@ def tile_allgnn_pa_v_kernel(tc, x, adj, W_in, b_in, deg, grad_out, out_0, out_1)
 
         dh, gq, xq, kq, acc = {}, {}, {}, {}, {}
 
-        def dh_mul(g, a, ts=range(4)):
-            for t in ts:
+        def dh_mul(g, a):
+            for t in range(4):
                 if g == 0:
                     dh[t] = bank("dh" + str(t))
                 mm(dh[t], gq[g], t, E5, a, E4, g == 0, g == NB - 1)
+
+        def dh_four(g, a, qs=range(4)):
+            for q in qs:
+                if g == 0:
+                    dh[q] = bank("dh" + str(q))
+                for t in range(4):
+                    first_pass, last_pass = g == 0 and t == 0, g == NB - 1 and t == 3
+                    mm(dh[q][:, P * t : P * (t + 1)], gq[g], t, E5, part(a, P * q, P * (q + 1)), E4, first_pass, last_pass)
+
+        def evict_four(dst):
+            for q in range(4):
+                nc.scalar.copy(
+                    out=dst.rearrange("p (s r t) -> p s r t", s=4, t=4)[:, :, 32 * q : 32 * (q + 1), :],
+                    in_=dh[q][:].rearrange("p (t r s) -> p s r t", t=4, s=4),
+                )
+
+        def flip_four(src):
+            words = src.bitcast(F32)
+            out = []
+            for u in range(2):
+                xt = bank("w" + str(u))
+                for s in range(4):
+                    nc.tensor.transpose(xt[:, P * s : P * (s + 1)], words[:, H * s + u : H * (s + 1) : 2], ident[:])
+                out.append(xt)
+            return out
+
+        def flip_four_copy(dst, xts, u):
+            nc.scalar.copy(
+                out=dst[:, 2 * B * u : 2 * B * (u + 1)].rearrange("p (c s) -> p c s", s=4),
+                in_=xts[u][:].bitcast(BF16).rearrange("p (s c) -> p c s", s=4),
+            )
 
         gall = codes("g", 1, NB)
         for g in range(NB):
@@ -239,8 +271,8 @@ def tile_allgnn_pa_v_kernel(tc, x, adj, W_in, b_in, deg, grad_out, out_0, out_1)
             return transposes(tags, lambda t, u: words[:, H * t + P * u : H * t + P * (u + 1)])
 
         def flip_copy(dst, xts, b, eng="S"):
-            dv = dst.bitcast(F32).rearrange("p (b t m u) -> p b t m u", b=2, t=2, u=2)
-            copy(eng, dv[:, b], xts[b].rearrange("p t u m -> p t m u"))
+            dv = dst.bitcast(F32).rearrange("p (b m t u) -> p b m t u", b=2, t=2, u=2)
+            copy(eng, dv[:, b], xts[b].rearrange("p t u m -> p m t u"))
 
         def dx_mul(h, b, tag, whole=True):
             o = bank(tag)
@@ -278,19 +310,19 @@ def tile_allgnn_pa_v_kernel(tc, x, adj, W_in, b_in, deg, grad_out, out_0, out_1)
             t = out_half(a)
             copy(
                 eng,
-                t.rearrange("p (m t) -> p m t", t=4),
-                acc[a][:].rearrange("p (t m) -> p m t", t=4),
+                t.rearrange("p (m u e) -> p m u e", u=2, e=2),
+                acc[a][:].rearrange("p (u m e) -> p m u e", u=2, e=2),
             )
             nc.sync.dma_start(out=out_1[P * a : P * (a + 1), :], in_=t)
 
         kh, p1 = pair(), pair()
         d = evict()
-        dh_mul(0, quant1(half(p0, 0), "one", 4, E4))
+        dh_four(0, quant1(half(p0, 0), "one", 4, E4))
         interleave("V", half(p1, 0), second[1][0], 0, B)
         xts = flip(d, ["w0", "w1"])
-        dh_mul(1, quant1(half(p0, 1), "one", 4, E4))
+        dh_four(1, quant1(half(p0, 1), "one", 4, E4))
         w_banks = transposes(["w2", "w3"], lambda a, u: w_words[:, a, u : HID // 2 : 2])
-        dh_mul(2, quant1(half(p1, 0), "one", 4, E4))
+        dh_four(2, quant1(half(p1, 0), "one", 4, E4))
         inter_h(half(kh, 1), d)
         interleave("S", half(p1, 1), second[1][1], 0, B)
         p0, p2 = pair(), pair()
@@ -302,8 +334,8 @@ def tile_allgnn_pa_v_kernel(tc, x, adj, W_in, b_in, deg, grad_out, out_0, out_1)
             flip_copy(half(kh, 0), xts, b)
         for b in range(2):
             nc.scalar.copy(out=dv[:, b], in_=w_banks[b].rearrange("p a u i -> p i a u"))
-        dh_mul(3, quant1(half(p1, 1), "one", 4, E4))
-        dh_mul(4, quant1(half(p2, 0), "one", 4, E4))
+        dh_four(3, quant1(half(p1, 1), "one", 4, E4))
+        dh_four(4, quant1(half(p2, 0), "one", 4, E4))
         wq = [quant1(w_ilv, "w", 1, E4)]
         shared(half(p0, 0), first[2][0], ONE)
         interleave("V", half(p0, 1), first[2][1], 0, B)
@@ -311,10 +343,11 @@ def tile_allgnn_pa_v_kernel(tc, x, adj, W_in, b_in, deg, grad_out, out_0, out_1)
         load_chunk(3)
 
         for c in range(2, NB):
-            d = evict()
+            evict_four(half(kh, 1))
+            mul = dh_mul if c == NB - 1 else dh_four
             if c == 2:
                 a = [quant1(half(p0, i), "one", 4, E4) for i in range(2)]
-                dh_mul(0, a[0])
+                mul(0, a[0])
                 for b in range(2):
                     dx_store(0, b, early[b])
                 late = [dx_mul(h, b + 2, "w" + str(b)) for b in range(2)]
@@ -322,61 +355,60 @@ def tile_allgnn_pa_v_kernel(tc, x, adj, W_in, b_in, deg, grad_out, out_0, out_1)
                 interleave("S", half(p1, 1), second[c][1], TWO, B)
             else:
                 a = quant2(p0, "two", 2, E4)
-                dh_mul(0, a[0])
+                mul(0, a[0])
             for b in range(2):
                 dx_store(c - 2, b + 2, late[b])
-            interleave("V", half(p1, 0), second[c][0], 0, B if c == 2 else MID)
+            interleave("V", half(p1, 0), second[c][0], 0, B)
             interleave("V", half(p1, 1), second[c][1], 0, TWO if c == 2 else B)
-            dh_mul(1, a[1])
-            xts = flip(d, ["w0", "w1"])
+            mul(1, a[1])
+            xts = flip_four(half(kh, 1))
             if c == NB - 1:
                 break
             p0, p2 = pair(), pair()
             interleave("V", half(p2, 0), last[c], 0, B)
             a = quant2(p1, "two", 2, E4)
-            dh_mul(2, a[0])
-            dh_mul(3, a[1])
-            inter_h(half(kh, 1), d)
-            interleave("S", half(p0, 0), first[c + 1][0], 0, B)
+            dh_four(2, a[0])
+            dh_four(3, a[1])
+            interleave("S", half(p0, 0), first[c + 1][0], 0, CUT)
             interleave("V", half(p2, 1), xraw[c - 2], 0, B)
             kq[c - 2], h = quant2(kh, "kh", 3, E5)
             kh = pair()
             for b in range(2):
-                flip_copy(half(kh, 0), xts, b)
-            interleave("S", half(p0, 1), first[c + 1][1], 0, B)
+                flip_four_copy(half(kh, 0), xts, b)
+            interleave("S", half(p0, 0), first[c + 1][0], CUT, B)
+            interleave("S", half(p0, 1), first[c + 1][1], MID, B)
             p1 = pair()
-            interleave("S", half(p1, 0), second[c + 1][0], MID, B)
-            o = [dx_mul(h, b, "w" + str(b)) for b in range(2)]
+            o = [dx_mul(h, b, "w" + str(b), False) for b in range(2)]
+            interleave("V", half(p0, 1), first[c + 1][1], 0, MID)
             a4, xq[c - 2] = quant2(p2, "ax", 2, E4)
-            dh_mul(4, a4)
+            dh_four(4, a4)
             if c + 2 < NB:
                 load_chunk(c + 2)
             for b in range(2):
                 dx_store(c - 1, b, o[b])
-            late = [dx_mul(h, b + 2, "w" + str(b)) for b in range(2)]
+            late = [dx_mul(h, b + 2, "w" + str(b), False) for b in range(2)]
             dw_mul(0, c - 2)
             dw_mul(1, c - 2)
 
         c = NB - 1
         p2, xx = pair(), pair()
-        interleave("S", half(p2, 0), last[c], 0, B)
-        interleave("V", half(p2, 1), xraw[c - 2], X2S, B)
+        shared(half(p2, 0), last[c], LAST)
         a = quant2(p1, "two", 2, E4)
         dh_mul(2, a[0])
         dh_mul(3, a[1])
-        inter_h(half(kh, 1), d)
+        interleave("V", half(p2, 1), xraw[c - 2], 0, B)
         interleave("V", half(xx, 0), xraw[c - 1], 0, H)
         kq[c - 2], h = quant2(kh, "kh", 3, E5)
         kh = pair()
         for b in range(2):
-            flip_copy(half(kh, 0), xts, b)
-        o = [dx_mul(h, b, "w" + str(b)) for b in range(2)]
+            flip_four_copy(half(kh, 0), xts, b)
+        o = [dx_mul(h, b, "w" + str(b), False) for b in range(2)]
         dh_mul(4, quant1(half(p2, 0), "one", 4, E4))
-        interleave("S", half(p2, 1), xraw[c - 2], 0, X2S)
+        interleave("S", half(xx, 1), xraw[c], 0, H)
         interleave("V", half(xx, 0), xraw[c - 1], H, B)
         for b in range(2):
             dx_store(c - 1, b, o[b])
-        late = [dx_mul(h, b + 2, "w" + str(b)) for b in range(2)]
+        late = [dx_mul(h, b + 2, "w" + str(b), False) for b in range(2)]
 
         xq[c - 2] = quant1(half(p2, 1), "x2", 1, E4)
         d = new([P, 4 * B], BF16, "d", 3)
@@ -431,9 +463,8 @@ def tile_allgnn_pa_v_kernel(tc, x, adj, W_in, b_in, deg, grad_out, out_0, out_1)
         def x_last(u):
             quant(part(xq[c], H * u, H * (u + 1)), xl[:, 4 * H * u : 4 * H * (u + 1)], E4)
 
-        interleave("V", xl, xraw[c], 0, H)
-        kq[c] = quant1(half(kl, 0), "kl", 1, E5)
         x_last(0)
+        kq[c] = quant1(half(kl, 0), "kl", 1, E5)
         interleave("V", xl, xraw[c], H, B)
         for k in range(NB - 2):
             dw_mul(3, k)

@@ -30,6 +30,8 @@ LAST = 160
 LAG = 2
 GV = 40
 AV = 256
+XA = 0
+XB = 0
 
 
 def tile_allgnn_pa_v_kernel(tc, x, adj, W_in, b_in, deg, grad_out, out_0, out_1):
@@ -91,15 +93,15 @@ def tile_allgnn_pa_v_kernel(tc, x, adj, W_in, b_in, deg, grad_out, out_0, out_1)
         def half(t, i):
             return t[:, 4 * B * i : 4 * B * (i + 1)]
 
-        def interleave(eng, dst, src, lo, hi):
+        def interleave(eng, dst, src, lo, hi, base=0):
             if eng == "S":
                 nc.scalar.copy(
-                    out=dst[:, 4 * lo : 4 * hi].rearrange("p (w i j) -> p w j i", i=RUN, j=4),
+                    out=dst[:, 4 * (lo - base) : 4 * (hi - base)].rearrange("p (w i j) -> p w j i", i=RUN, j=4),
                     in_=src[:, :, lo:hi].rearrange("p j (w i) -> p w j i", i=RUN),
                 )
             else:
                 nc.vector.tensor_copy(
-                    out=dst[:, 4 * lo : 4 * hi].rearrange("p (w h i j) -> p h w j i", h=2, i=RUN, j=4),
+                    out=dst[:, 4 * (lo - base) : 4 * (hi - base)].rearrange("p (w h i j) -> p h w j i", h=2, i=RUN, j=4),
                     in_=src[:, :, lo:hi].rearrange("p j (w h i) -> p h w j i", h=2, i=RUN),
                 )
 
@@ -188,11 +190,11 @@ def tile_allgnn_pa_v_kernel(tc, x, adj, W_in, b_in, deg, grad_out, out_0, out_1)
                     in_=dh[q][:].rearrange("p (t r s) -> p s r t", t=4, s=4),
                 )
 
-        def flip_four(src):
+        def flip_four(src, tags=("w0", "w1")):
             words = src.bitcast(F32)
             out = []
             for u in range(2):
-                xt = bank("w" + str(u))
+                xt = bank(tags[u])
                 for s in range(4):
                     nc.tensor.transpose(xt[:, P * s : P * (s + 1)], words[:, H * s + u : H * (s + 1) : 2], ident[:])
                 out.append(xt)
@@ -342,12 +344,14 @@ def tile_allgnn_pa_v_kernel(tc, x, adj, W_in, b_in, deg, grad_out, out_0, out_1)
         early = [dx_mul(h, b, "w" + str(b)) for b in range(2)]
         load_chunk(3)
 
-        for c in range(2, NB):
+        def quarter(t, i):
+            return t[:, 4 * H * i : 4 * H * (i + 1)]
+
+        for c in range(2, NB - 1):
             evict_four(half(kh, 1))
-            mul = dh_mul if c == NB - 1 else dh_four
             if c == 2:
                 a = [quant1(half(p0, i), "one", 4, E4) for i in range(2)]
-                mul(0, a[0])
+                dh_four(0, a[0])
                 for b in range(2):
                     dx_store(0, b, early[b])
                 late = [dx_mul(h, b + 2, "w" + str(b)) for b in range(2)]
@@ -355,35 +359,45 @@ def tile_allgnn_pa_v_kernel(tc, x, adj, W_in, b_in, deg, grad_out, out_0, out_1)
                 interleave("S", half(p1, 1), second[c][1], TWO, B)
             else:
                 a = quant2(p0, "two", 2, E4)
-                mul(0, a[0])
+                dh_four(0, a[0])
             for b in range(2):
                 dx_store(c - 2, b + 2, late[b])
             interleave("V", half(p1, 0), second[c][0], 0, B)
             interleave("V", half(p1, 1), second[c][1], 0, TWO if c == 2 else B)
-            mul(1, a[1])
+            dh_four(1, a[1])
             xts = flip_four(half(kh, 1))
-            if c == NB - 1:
-                break
             p0, p2 = pair(), pair()
             interleave("V", half(p2, 0), last[c], 0, B)
             a = quant2(p1, "two", 2, E4)
             dh_four(2, a[0])
             dh_four(3, a[1])
-            interleave("S", half(p0, 0), first[c + 1][0], 0, CUT)
+            if c == 2:
+                interleave("S", half(p0, 0), first[c + 1][0], 0, CUT)
+            else:
+                tail = first[c + 1] + second[c + 1]
+                interleave("S", quarter(p0, 0), tail[0], 0, H)
+                interleave("S", quarter(p0, 1), tail[1], 0, CUT - H)
             interleave("V", half(p2, 1), xraw[c - 2], 0, B)
             kq[c - 2], h = quant2(kh, "kh", 3, E5)
             kh = pair()
             for b in range(2):
                 flip_four_copy(half(kh, 0), xts, b)
-            interleave("S", half(p0, 0), first[c + 1][0], CUT, B)
-            interleave("S", half(p0, 1), first[c + 1][1], MID, B)
-            p1 = pair()
+            if c == 2:
+                interleave("S", half(p0, 0), first[c + 1][0], CUT, B)
+                interleave("S", half(p0, 1), first[c + 1][1], MID, B)
+            else:
+                interleave("S", quarter(p0, 1), tail[1], CUT - H, H)
+                interleave("S", quarter(p0, 2), tail[2], MID - H, H)
             o = [dx_mul(h, b, "w" + str(b), False) for b in range(2)]
-            interleave("V", half(p0, 1), first[c + 1][1], 0, MID)
+            if c == 2:
+                p1 = pair()
+                interleave("V", half(p0, 1), first[c + 1][1], 0, MID)
+                load_chunk(c + 2)
             a4, xq[c - 2] = quant2(p2, "ax", 2, E4)
             dh_four(4, a4)
-            if c + 2 < NB:
-                load_chunk(c + 2)
+            if c > 2:
+                interleave("V", quarter(p0, 3), tail[3], 0, H)
+                interleave("V", quarter(p0, 2), tail[2], 0, MID - H)
             for b in range(2):
                 dx_store(c - 1, b, o[b])
             late = [dx_mul(h, b + 2, "w" + str(b), False) for b in range(2)]
@@ -391,88 +405,121 @@ def tile_allgnn_pa_v_kernel(tc, x, adj, W_in, b_in, deg, grad_out, out_0, out_1)
             dw_mul(1, c - 2)
 
         c = NB - 1
-        p2, xx = pair(), pair()
-        shared(half(p2, 0), last[c], LAST)
-        a = quant2(p1, "two", 2, E4)
-        dh_mul(2, a[0])
-        dh_mul(3, a[1])
-        interleave("V", half(p2, 1), xraw[c - 2], 0, B)
-        interleave("V", half(xx, 0), xraw[c - 1], 0, H)
-        kq[c - 2], h = quant2(kh, "kh", 3, E5)
-        kh = pair()
-        for b in range(2):
-            flip_four_copy(half(kh, 0), xts, b)
-        o = [dx_mul(h, b, "w" + str(b), False) for b in range(2)]
-        dh_mul(4, quant1(half(p2, 0), "one", 4, E4))
-        interleave("S", half(xx, 1), xraw[c], 0, H)
-        interleave("V", half(xx, 0), xraw[c - 1], H, B)
-        for b in range(2):
-            dx_store(c - 1, b, o[b])
-        late = [dx_mul(h, b + 2, "w" + str(b), False) for b in range(2)]
+        wide = {}
 
-        xq[c - 2] = quant1(half(p2, 1), "x2", 1, E4)
+        def wide_pass(u, b, a, g, start, stop):
+            if start:
+                wide[u, b] = bank("dh" + str(2 * u + b))
+            for t in range(2):
+                mm(wide[u, b][:, H * t : H * (t + 1)], gq[g], 2 * b + t, E5, a, E4, start and t == 0, stop and t == 1)
+
         d = new([P, 4 * B], BF16, "d", 3)
 
-        def evict_half(u, engs):
-            for t in range(4):
-                copy(
-                    engs[t],
-                    d[:, B * t + H * u : B * t + H * (u + 1)].rearrange("p (m e) -> p m e", e=2),
-                    dh[t][:].rearrange("p (m u e) -> p u m e", u=2, e=2)[:, u],
-                )
-
-        def inter_h_half(dst, u):
-            nc.vector.tensor_copy(
-                out=dst[:, 2 * B * u : 2 * B * (u + 1)].rearrange("p (e m t) -> p m t e", e=2, t=4),
-                in_=d[:].rearrange("p (t u m e) -> p u m t e", t=4, u=2, e=2)[:, u],
+        def evict_wide(u, b, eng):
+            copy(
+                eng,
+                d[:].rearrange("p (t v m e) -> p t v m e", t=4, v=2, e=2)[:, 2 * b : 2 * b + 2, :, 64 * u : 64 * (u + 1), :],
+                wide[u, b][:].rearrange("p (t m v e) -> p t v m e", t=2, v=2, e=2),
             )
 
-        hq = part(codes("one", 4, 1), 0, B)
-        hi = half(kh, 1)
+        def inter_half(dst, u):
+            nc.vector.tensor_copy(
+                out=dst.rearrange("p (e m v t) -> p m v t e", e=2, v=2, t=4),
+                in_=d[:].rearrange("p (t v m e) -> p m v t e", t=4, v=2, e=2)[:, 64 * u : 64 * (u + 1)],
+            )
 
-        def dx_half(u):
-            quant(part(hq, H * u, H * (u + 1)), hi[:, 4 * H * u : 4 * H * (u + 1)], E5)
-            return [dx_mul(hq, b, ("w", "dh")[u] + str(b % 2), False) for b in (2 * u, 2 * u + 1)]
+        def dx_last(u, e, o, eng):
+            t = out_half(e)
+            copy(eng, t, o[:])
+            lo = B * c + H * u
+            nc.sync.dma_start(out=out_0[lo : lo + H, :].rearrange("(p e) w -> p e w", e=2)[:, e, :], in_=t)
 
-        dw_mul(0, c - 2)
-        dw_mul(1, c - 2)
-        evict_half(0, "SVSV")
-        evict_half(1, "SSSS")
-        kq[c - 1] = quant1(half(kh, 0), "one", 4, E5)
-        inter_h_half(hi, 0)
-        xq[c - 1] = quant1(half(xx, 0), "one", 4, E4)
+        def dw_sum(a, k, tag=None, stop=False):
+            if tag:
+                acc[a] = bank(tag)
+            mm(acc[a], xq[k], a, E4, kq[k], E5, tag is not None, stop)
+
+        evict_four(half(kh, 1))
+        p1, p2 = pair(), pair()
+        interleave("V", quarter(p1, 0), tail[0], H, B, H)
+        pa = part(codes("two", 2, 2), 0, 2 * B)
+        quant(pa, p0[:], E4)
         for b in range(2):
-            dx_store(c - 1, b + 2, late[b])
-        xts = flip(d, ["dh0", "dh1"])
-        kl = pair()
-        flip_copy(half(kl, 0), xts, 0)
-        dw_mul(2, 0)
-        dw_mul(2, 1)
-        o = dx_half(0)
-        inter_h_half(hi, 1)
-        flip_copy(half(kl, 0), xts, 1, "V")
-        dw_mul(2, 2)
-        dw_mul(0, c - 1)
-        dw_mul(1, c - 1)
-        o.extend(dx_half(1))
-        for b in range(4):
-            dx_store(c, b, o[b])
+            for g in range(4):
+                wide_pass(0, b, part(pa, H * g, H * (g + 1)), g, g == 0, False)
+        for b in range(2):
+            dx_store(c - 2, b + 2, late[b])
+        interleave("V", half(p2, 0), last[c], 0, B)
+        interleave("V", quarter(p1, 1), tail[1], H, B, H)
+        interleave("S", quarter(p1, 3), tail[3], H, B, H)
+        a4 = quant1(half(p2, 0), "one", 4, E4)
+        for b in range(2):
+            wide_pass(0, b, part(a4, 0, H), NB - 1, False, True)
+        xts3 = flip_four(half(kh, 1))
+        kq[c - 2], h = quant2(kh, "kh", 3, E5)
+        pb = part(codes("two", 2, 2), 0, 2 * B)
+        quant(part(pb, 0, B), half(p1, 0), E4)
+        for b in range(2):
+            wide_pass(1, b, part(a4, H, B), NB - 1, True, False)
+        for g in range(2):
+            for b in range(2):
+                wide_pass(1, b, part(pb, H * g, H * (g + 1)), g, False, False)
+        for b in range(2):
+            evict_wide(0, b, "S")
+        o = [dx_mul(h, b, "dh" + str(b), False) for b in range(2)]
+        hi, xx, kk = pair(), pair(), pair()
+        interleave("V", quarter(p1, 2), tail[2], H, B, H)
+        interleave("V", half(p2, 1), xraw[c - 2], 0, H)
+        quant(part(pb, B, 2 * B), half(p1, 1), E4)
+        for b in range(2):
+            for g in range(2, 4):
+                wide_pass(1, b, part(pb, H * g, H * (g + 1)), g, False, g == 3)
+        for u in range(2):
+            flip_four_copy(half(kk, 0), xts3, u)
+        for b in range(2):
+            dx_store(c - 1, b, o[b])
+        o = [dx_mul(h, b + 2, "w" + str(b), False) for b in range(2)]
+        hq = part(codes("one", 4, 1), 0, B)
+        inter_half(quarter(hi, 0), 0)
+        interleave("V", half(p2, 1), xraw[c - 2], H, B)
+        quant(part(hq, 0, H), quarter(hi, 0), E5)
+        xq[c - 2] = quant1(half(p2, 1), "x2", 1, E4)
+        dw_sum(0, c - 2)
+        dw_sum(1, c - 2)
+        evict_wide(1, 1, "V")
+        evict_wide(1, 0, "S")
+        for k in range(3):
+            dw_sum(2, k, "dh0" if k == 0 else None)
+        xts = flip(d, ["dh2", "dh3"])
+        for b in range(2):
+            dx_store(c - 1, b + 2, o[b])
+        oa = [dx_mul(hq, e, "w" + str(e), False) for e in range(2)]
+        for k in range(3):
+            dw_sum(3, k, "dh1" if k == 0 else None)
+        kq[c - 1] = quant1(half(kk, 0), "one", 4, E5)
+        inter_half(quarter(hi, 1), 1)
+        interleave("V", half(xx, 0), xraw[c - 1], 0, B)
+        quant(part(hq, H, B), quarter(hi, 1), E5)
+        flip_copy(half(kk, 1), xts, 0, "S")
+        flip_copy(half(kk, 1), xts, 1, "S")
+        for e in range(2):
+            dx_last(0, e, oa[e], "S")
+        ob = [dx_mul(hq, 2 + e, "dh" + str(2 + e), False) for e in range(2)]
+        xq[c - 1] = quant1(half(xx, 0), "one", 4, E4)
+        for a in range(4):
+            dw_sum(a, c - 1)
         xl = half(xx, 1)
         xq[c] = part(codes("xl", 1, 1), 0, B)
-
-        def x_last(u):
-            quant(part(xq[c], H * u, H * (u + 1)), xl[:, 4 * H * u : 4 * H * (u + 1)], E4)
-
-        x_last(0)
-        kq[c] = quant1(half(kl, 0), "kl", 1, E5)
+        interleave("V", xl, xraw[c], 0, H)
+        kq[c] = quant1(half(kk, 1), "kl", 1, E5)
+        for e in range(2):
+            dx_last(1, e, ob[e], "S")
+        quant(part(xq[c], 0, H), quarter(xl, 0), E4)
         interleave("V", xl, xraw[c], H, B)
-        for k in range(NB - 2):
-            dw_mul(3, k)
-        dw_mul(0, c)
-        dw_mul(1, c)
-        x_last(1)
-        for a in (2, 3):
-            dw_mul(a, c - 1)
-            dw_mul(a, c)
+        dw_sum(0, c, stop=True)
+        dw_sum(1, c, stop=True)
+        quant(part(xq[c], H, B), quarter(xl, 1), E4)
+        dw_sum(2, c, stop=True)
+        dw_sum(3, c, stop=True)
         for a in range(4):
-            dw_store(a, "SV"[a % 2])
+            dw_store(a, "SSVS"[a])

@@ -28,6 +28,7 @@ MID = 288
 CUT = 384
 LAST = 160
 LAG = 2
+XV = 256
 GV = 40
 AV = 256
 XA = 0
@@ -169,10 +170,10 @@ def tile_allgnn_pa_v_kernel(tc, x, adj, W_in, b_in, deg, grad_out, out_0, out_1)
 
         dh, gq, xq, kq, acc = {}, {}, {}, {}, {}
 
-        def dh_mul(g, a):
+        def dh_mul(g, a, dh=dh, tag="dh"):
             for t in range(4):
                 if g == 0:
-                    dh[t] = bank("dh" + str(t))
+                    dh[t] = bank(tag + str(t))
                 mm(dh[t], gq[g], t, E5, a, E4, g == 0, g == NB - 1)
 
         def dh_four(g, a, qs=range(4)):
@@ -210,14 +211,14 @@ def tile_allgnn_pa_v_kernel(tc, x, adj, W_in, b_in, deg, grad_out, out_0, out_1)
         for g in range(NB):
             gq[g] = part(gall, B * g, B * (g + 1))
 
-        tiles = []
+        tiles, dh0 = [], {}
 
         def finish(i):
             kind, g = head[i]
             if kind == "g":
                 quant(gq[g], tiles[i], E5)
             else:
-                dh_mul(g, quant1(tiles[i], "one", 4, E4))
+                dh_mul(g, quant1(tiles[i], "one", 4, E4), dh0, "w")
 
         for i, (kind, g) in enumerate(head):
             if i % 2 == 0:
@@ -253,7 +254,7 @@ def tile_allgnn_pa_v_kernel(tc, x, adj, W_in, b_in, deg, grad_out, out_0, out_1)
 
         w_words = w_raw[:].bitcast(F32)
 
-        def evict():
+        def evict(dh):
             d = new([P, 4 * B], BF16, "d", 3)
             for t in range(4):
                 nc.scalar.copy(
@@ -318,7 +319,7 @@ def tile_allgnn_pa_v_kernel(tc, x, adj, W_in, b_in, deg, grad_out, out_0, out_1)
             nc.sync.dma_start(out=out_1[P * a : P * (a + 1), :], in_=t)
 
         kh, p1 = pair(), pair()
-        d = evict()
+        d = evict(dh0)
         dh_four(0, quant1(half(p0, 0), "one", 4, E4))
         interleave("V", half(p1, 0), second[1][0], 0, B)
         xts = flip(d, ["w0", "w1"])
@@ -486,40 +487,45 @@ def tile_allgnn_pa_v_kernel(tc, x, adj, W_in, b_in, deg, grad_out, out_0, out_1)
         xq[c - 2] = quant1(half(p2, 1), "x2", 1, E4)
         dw_sum(0, c - 2)
         dw_sum(1, c - 2)
+        interleave("V", half(xx, 0), xraw[c - 1], 0, H)
         evict_wide(1, 1, "V")
         evict_wide(1, 0, "S")
-        for k in range(3):
-            dw_sum(2, k, "dh0" if k == 0 else None)
-        xts = flip(d, ["dh2", "dh3"])
         for b in range(2):
             dx_store(c - 1, b + 2, o[b])
-        oa = [dx_mul(hq, e, "w" + str(e), False) for e in range(2)]
-        for k in range(3):
-            dw_sum(3, k, "dh1" if k == 0 else None)
-        kq[c - 1] = quant1(half(kk, 0), "one", 4, E5)
-        inter_half(quarter(hi, 1), 1)
-        interleave("V", half(xx, 0), xraw[c - 1], 0, B)
-        quant(part(hq, H, B), quarter(hi, 1), E5)
-        flip_copy(half(kk, 1), xts, 0, "S")
-        flip_copy(half(kk, 1), xts, 1, "S")
+        dw_sum(2, 0, "dh0")
+        oa = [dx_mul(hq, 0, "w0", False)]
+        dw_sum(2, 1)
+        oa.append(dx_mul(hq, 1, "w1", False))
+        xts = flip(d, ["dh2", "dh3"])
         for e in range(2):
             dx_last(0, e, oa[e], "S")
-        ob = [dx_mul(hq, 2 + e, "dh" + str(2 + e), False) for e in range(2)]
-        xq[c - 1] = quant1(half(xx, 0), "one", 4, E4)
-        for a in range(4):
-            dw_sum(a, c - 1)
+        kq[c - 1] = quant1(half(kk, 0), "one", 4, E5)
+        inter_half(quarter(hi, 1), 1)
+        interleave("V", half(xx, 0), xraw[c - 1], H, B)
+        quant(part(hq, H, B), quarter(hi, 1), E5)
+        dw_sum(2, 2)
+        ob = [dx_mul(hq, 2 + e, "w" + str(e), False) for e in range(2)]
+        for k in range(3):
+            dw_sum(3, k, "dh1" if k == 0 else None)
+        for b in range(2):
+            flip_copy(half(kk, 1), xts, b, "S")
         xl = half(xx, 1)
-        xq[c] = part(codes("xl", 1, 1), 0, B)
-        interleave("V", xl, xraw[c], 0, H)
+        interleave("V", xl, xraw[c], 0, XV)
+        xq[c - 1] = quant1(half(xx, 0), "one", 4, E4)
+        dx_last(1, 0, ob[0], "S")
+        interleave("S", xl, xraw[c], XV, B)
         kq[c] = quant1(half(kk, 1), "kl", 1, E5)
-        for e in range(2):
-            dx_last(1, e, ob[e], "S")
+        xq[c] = part(codes("xl", 1, 1), 0, B)
         quant(part(xq[c], 0, H), quarter(xl, 0), E4)
-        interleave("V", xl, xraw[c], H, B)
-        dw_sum(0, c, stop=True)
-        dw_sum(1, c, stop=True)
+        for a in range(2):
+            dw_sum(a, c - 1)
+        for a in range(2):
+            dw_sum(a, c, stop=True)
+        dx_last(1, 1, ob[1], "V")
         quant(part(xq[c], H, B), quarter(xl, 1), E4)
-        dw_sum(2, c, stop=True)
-        dw_sum(3, c, stop=True)
+        for a in range(2, 4):
+            dw_sum(a, c - 1)
+        for a in range(2, 4):
+            dw_sum(a, c, stop=True)
         for a in range(4):
-            dw_store(a, "SSVS"[a])
+            dw_store(a, "SVSV"[a])

from contextlib import ExitStack

import concourse.mybir as mybir
from concourse.masks import make_identity

N = 2560
IN = 512
HID = 512
FLOPS = 2 * (N * N * HID + 2 * N * IN * HID)
BYTES = 2 * (N * IN + N * N + IN * HID + N * HID) + 4 * (N + N * IN + IN * HID)

F32 = mybir.dt.float32
BF16 = mybir.dt.bfloat16
U32 = mybir.dt.uint32
U8 = mybir.dt.uint8
E4 = mybir.dt.float8_e4m3fn_x4
E5 = mybir.dt.float8_e5m2_x4

P = 128
B = 512
NB = N // B
H = B // 2
RUN = 8
HEAD = 128
ONE = 96
TWO = 416
MID = 288
CUT = 384
LAST = 160
LAG = 2
XV = 256
GV = 40
AV = 256
XA = 0
XB = 0


def tile_allgnn_pa_v_kernel(tc, x, adj, W_in, b_in, deg, grad_out, out_0, out_1):
    nc = tc.nc
    with ExitStack() as ctx:
        sb = ctx.enter_context(tc.tile_pool(name="sb", bufs=1))
        ps = ctx.enter_context(tc.psum_pool(name="ps", bufs=1))
        ctx.enter_context(tc.manual_schedule())

        def new(shape, dt, tag, bufs):
            return sb.tile(shape, dt, tag=tag, name=tag, bufs=bufs, align_bytes=64)

        def bank(tag):
            return ps.tile([P, B], F32, tag=tag, name=tag, bufs=1)

        def codes(tag, bufs, n):
            return new([P, n * B], U32, tag + "c", bufs), new([P, n * B], U8, tag + "s", bufs)

        def quant(dst, src, fmt):
            nc.vector.quantize_mx(out=dst[0].bitcast(fmt), scales=dst[1], in_=src)

        def part(cs, lo, hi):
            return cs[0][:, lo:hi], cs[1][:, lo:hi]

        def quant1(src, tag, bufs, fmt):
            cs = part(codes(tag, bufs, 1), 0, B)
            quant(cs, src, fmt)
            return cs

        def quant2(src, tag, bufs, fmt):
            cs = codes(tag, bufs, 2)
            quant(part(cs, 0, 2 * B), src[:], fmt)
            return part(cs, 0, B), part(cs, B, 2 * B)

        def mm(out, l, blk, lfmt, r, rfmt, start, stop):
            cols = slice(P * blk, P * (blk + 1))
            nc.tensor.matmul_mx(
                out=out[:],
                lhsT=l[0][:, cols].bitcast(lfmt),
                lhsT_scale=l[1][:, cols],
                rhs=r[0].bitcast(rfmt),
                rhs_scale=r[1],
                start=start,
                stop=stop,
            )

        def rows(ap, g, cols):
            return ap[B * g : B * (g + 1), cols].rearrange("(p j) w -> p j w", j=4)

        def copy(eng, out, in_):
            if eng == "S":
                nc.scalar.copy(out=out, in_=in_)
            else:
                nc.vector.tensor_copy(out=out, in_=in_)

        def pair():
            return new([P, 8 * B], BF16, "ilv", 6)

        def half(t, i):
            return t[:, 4 * B * i : 4 * B * (i + 1)]

        def interleave(eng, dst, src, lo, hi, base=0):
            if eng == "S":
                nc.scalar.copy(
                    out=dst[:, 4 * (lo - base) : 4 * (hi - base)].rearrange("p (w i j) -> p w j i", i=RUN, j=4),
                    in_=src[:, :, lo:hi].rearrange("p j (w i) -> p w j i", i=RUN),
                )
            else:
                nc.vector.tensor_copy(
                    out=dst[:, 4 * (lo - base) : 4 * (hi - base)].rearrange("p (w h i j) -> p h w j i", h=2, i=RUN, j=4),
                    in_=src[:, :, lo:hi].rearrange("p j (w h i) -> p h w j i", h=2, i=RUN),
                )

        def load(ap, g, c=0):
            t = new([P, 4, B], BF16, "raw", 15)
            nc.sync.dma_start(out=t[:], in_=rows(ap, g, slice(B * c, B * (c + 1))))
            return t

        r = new([P, NB, 4], F32, "deg", 1)
        nc.sync.dma_start(out=r[:], in_=deg.rearrange("(g p j) -> p g j", p=P, j=4))
        ident = new([P, P], F32, "ident", 1)
        make_identity(nc, ident[:])

        graw, a0raw, first, second, last, xraw = {}, {}, {}, {}, {}, {}
        graw[0] = new([P, 4, B], BF16, "raw", 15)
        for j in (0, 2):
            nc.sync.dma_start(out=graw[0][:, j : j + 2, :], in_=rows(grad_out, 0, slice(0, HID))[:, j : j + 2, :])
        head = [("g", 0), ("g", 1)]
        for g in range(NB):
            if g + 2 < NB:
                head.append(("g", g + 2))
            head.append(("a", g))
        for kind, g in head[1:]:
            if kind == "g":
                graw[g] = load(grad_out, g)
            else:
                a0raw[g] = load(adj, g)
        first[1] = [load(adj, g, 1) for g in range(2)]
        w_raw = new([P, 4, HID], BF16, "wraw", 1)

        def load_chunk(c):
            second[c] = [load(adj, g, c) for g in (2, 3)]
            if c == 1:
                nc.sync.dma_start(out=w_raw[:], in_=W_in.rearrange("(p a) h -> p a h", a=4))
            last[c] = load(adj, NB - 1, c)
            if c + 1 < NB:
                first[c + 1] = [load(adj, 0, c + 1)]
            if c >= 2:
                xraw[c - 2] = load(x, c - 2)
            if c + 1 < NB:
                first[c + 1].append(load(adj, 1, c + 1))
            else:
                for k in range(c - 1, NB):
                    xraw[k] = load(x, k)

        nc.vector.tensor_scalar_add(r[:], r[:], 1.0)
        rec = new([P, NB, 4], F32, "rec", 1)
        nc.vector.reciprocal(out=rec[:], in_=r[:])

        def scale_g(g):
            t = new([P, 4, HID], BF16, "d", 3)
            for j in range(4):
                nc.vector.tensor_scalar_mul(t[:, j, :], graw[g][:, j, :], rec[:, g, j : j + 1])
            return t

        def inter_g(dst, src):
            dv = dst.rearrange("p (t m u e) -> p m u t e", t=4, u=2, e=2)
            sv = src[:].rearrange("p (u e) (m t) -> p m u t e", u=2, t=4)
            nc.scalar.copy(out=dv[:, GV:], in_=sv[:, GV:])
            nc.vector.tensor_copy(out=dv[:, :GV], in_=sv[:, :GV])

        def shared(dst, src, cut):
            interleave("S", dst, src, cut, B)
            interleave("V", dst, src, 0, cut)

        dh, gq, xq, kq, acc = {}, {}, {}, {}, {}

        def dh_mul(g, a, dh=dh, tag="dh"):
            for t in range(4):
                if g == 0:
                    dh[t] = bank(tag + str(t))
                mm(dh[t], gq[g], t, E5, a, E4, g == 0, g == NB - 1)

        def dh_four(g, a, qs=range(4)):
            for q in qs:
                if g == 0:
                    dh[q] = bank("dh" + str(q))
                for t in range(4):
                    first_pass, last_pass = g == 0 and t == 0, g == NB - 1 and t == 3
                    mm(dh[q][:, P * t : P * (t + 1)], gq[g], t, E5, part(a, P * q, P * (q + 1)), E4, first_pass, last_pass)

        def evict_four(dst):
            for q in range(4):
                nc.scalar.copy(
                    out=dst.rearrange("p (s r t) -> p s r t", s=4, t=4)[:, :, 32 * q : 32 * (q + 1), :],
                    in_=dh[q][:].rearrange("p (t r s) -> p s r t", t=4, s=4),
                )

        def flip_four(src, tags=("w0", "w1")):
            words = src.bitcast(F32)
            out = []
            for u in range(2):
                xt = bank(tags[u])
                for s in range(4):
                    nc.tensor.transpose(xt[:, P * s : P * (s + 1)], words[:, H * s + u : H * (s + 1) : 2], ident[:])
                out.append(xt)
            return out

        def flip_four_copy(dst, xts, u):
            nc.scalar.copy(
                out=dst[:, 2 * B * u : 2 * B * (u + 1)].rearrange("p (c s) -> p c s", s=4),
                in_=xts[u][:].bitcast(BF16).rearrange("p (s c) -> p c s", s=4),
            )

        gall = codes("g", 1, NB)
        for g in range(NB):
            gq[g] = part(gall, B * g, B * (g + 1))

        tiles, dh0 = [], {}

        def finish(i):
            kind, g = head[i]
            if kind == "g":
                quant(gq[g], tiles[i], E5)
            else:
                dh_mul(g, quant1(tiles[i], "one", 4, E4), dh0, "w")

        for i, (kind, g) in enumerate(head):
            if i % 2 == 0:
                t = pair()
                tiles.extend([half(t, 0), half(t, 1)])
            if kind == "g":
                s = scale_g(g)
            if i >= LAG:
                finish(i - LAG)
            if kind == "g":
                inter_g(tiles[i], s)
            else:
                shared(tiles[i], a0raw[g], AV)
            if i == NB:
                load_chunk(1)
        for i in range(len(head) - LAG, len(head) - 1):
            finish(i)
        p0 = pair()
        shared(half(p0, 0), first[1][0], HEAD)
        finish(len(head) - 1)
        interleave("V", half(p0, 1), first[1][1], 0, B)
        load_chunk(2)

        def transposes(tags, block):
            out = []
            for b in range(2):
                xt = bank(tags[b])[:].rearrange("p (t u m) -> p t u m", t=2, u=2)
                for t in range(2):
                    for u in range(2):
                        nc.tensor.transpose(xt[:, t, u, :], block(2 * b + t, u), ident[:])
                out.append(xt)
            return out

        w_words = w_raw[:].bitcast(F32)

        def evict(dh):
            d = new([P, 4 * B], BF16, "d", 3)
            for t in range(4):
                nc.scalar.copy(
                    out=d[:, B * t : B * (t + 1)].rearrange("p (u m e) -> p u m e", u=2, e=2),
                    in_=dh[t][:].rearrange("p (m u e) -> p u m e", u=2, e=2),
                )
            return d

        def inter_h(dst, d):
            nc.vector.tensor_copy(
                out=dst.rearrange("p (e w s t) -> p w s e t", e=2, s=2, t=2),
                in_=d[:].rearrange("p (s t w e) -> p w s e t", s=2, t=2, e=2),
            )

        def flip(d, tags):
            words = d[:].bitcast(F32)
            return transposes(tags, lambda t, u: words[:, H * t + P * u : H * t + P * (u + 1)])

        def flip_copy(dst, xts, b, eng="S"):
            dv = dst.bitcast(F32).rearrange("p (b m t u) -> p b m t u", b=2, t=2, u=2)
            copy(eng, dv[:, b], xts[b].rearrange("p t u m -> p m t u"))

        def dx_mul(h, b, tag, whole=True):
            o = bank(tag)
            mm(o, h, 2 * (b % 2) + b // 2 if whole else b, E5, wq[0], E4, True, True)
            return o

        waiting, stage = [], []

        def out_half(i):
            if i % 2 == 0:
                stage.append(new([P, 2, IN], F32, "out", 10))
            return stage[-1][:, i % 2, :]

        def flush():
            for dst, src in waiting:
                nc.sync.dma_start(out=dst, in_=src)
            waiting.clear()

        def dx_store(c, b, o):
            t = out_half(b)
            nc.scalar.copy(out=t, in_=o[:])
            if c == NB - 1:
                nc.sync.dma_start(out=rows(out_0, c, slice(0, IN))[:, b, :], in_=t)
            elif b % 2 == 1:
                waiting.append((rows(out_0, c, slice(0, IN))[:, b - 1 : b + 1, :], stage[-1][:]))
                if c > 0:
                    flush()

        def dw_mul(a, c):
            if c == 0:
                acc[a] = bank(("w" if a < 2 else "dh") + str(2 + a % 2))
            mm(acc[a], xq[c], a, E4, kq[c], E5, c == 0, c == NB - 1)

        def dw_store(a, eng):
            t = out_half(a)
            copy(
                eng,
                t.rearrange("p (m u e) -> p m u e", u=2, e=2),
                acc[a][:].rearrange("p (u m e) -> p m u e", u=2, e=2),
            )
            nc.sync.dma_start(out=out_1[P * a : P * (a + 1), :], in_=t)

        kh, p1 = pair(), pair()
        d = evict(dh0)
        dh_four(0, quant1(half(p0, 0), "one", 4, E4))
        interleave("V", half(p1, 0), second[1][0], 0, B)
        xts = flip(d, ["w0", "w1"])
        dh_four(1, quant1(half(p0, 1), "one", 4, E4))
        w_banks = transposes(["w2", "w3"], lambda a, u: w_words[:, a, u : HID // 2 : 2])
        dh_four(2, quant1(half(p1, 0), "one", 4, E4))
        inter_h(half(kh, 1), d)
        interleave("S", half(p1, 1), second[1][1], 0, B)
        p0, p2 = pair(), pair()
        interleave("V", half(p2, 0), last[1], 0, B)
        h = quant1(half(kh, 1), "h", 1, E5)
        dv = half(kh, 0).bitcast(F32).rearrange("p (i b a u) -> p b i a u", b=2, a=2, u=2)
        w_ilv, kh = half(kh, 0), pair()
        for b in range(2):
            flip_copy(half(kh, 0), xts, b)
        for b in range(2):
            nc.scalar.copy(out=dv[:, b], in_=w_banks[b].rearrange("p a u i -> p i a u"))
        dh_four(3, quant1(half(p1, 1), "one", 4, E4))
        dh_four(4, quant1(half(p2, 0), "one", 4, E4))
        wq = [quant1(w_ilv, "w", 1, E4)]
        shared(half(p0, 0), first[2][0], ONE)
        interleave("V", half(p0, 1), first[2][1], 0, B)
        early = [dx_mul(h, b, "w" + str(b)) for b in range(2)]
        load_chunk(3)

        def quarter(t, i):
            return t[:, 4 * H * i : 4 * H * (i + 1)]

        for c in range(2, NB - 1):
            evict_four(half(kh, 1))
            if c == 2:
                a = [quant1(half(p0, i), "one", 4, E4) for i in range(2)]
                dh_four(0, a[0])
                for b in range(2):
                    dx_store(0, b, early[b])
                late = [dx_mul(h, b + 2, "w" + str(b)) for b in range(2)]
                p1 = pair()
                interleave("S", half(p1, 1), second[c][1], TWO, B)
            else:
                a = quant2(p0, "two", 2, E4)
                dh_four(0, a[0])
            for b in range(2):
                dx_store(c - 2, b + 2, late[b])
            interleave("V", half(p1, 0), second[c][0], 0, B)
            interleave("V", half(p1, 1), second[c][1], 0, TWO if c == 2 else B)
            dh_four(1, a[1])
            xts = flip_four(half(kh, 1))
            p0, p2 = pair(), pair()
            interleave("V", half(p2, 0), last[c], 0, B)
            a = quant2(p1, "two", 2, E4)
            dh_four(2, a[0])
            dh_four(3, a[1])
            if c == 2:
                interleave("S", half(p0, 0), first[c + 1][0], 0, CUT)
            else:
                tail = first[c + 1] + second[c + 1]
                interleave("S", quarter(p0, 0), tail[0], 0, H)
                interleave("S", quarter(p0, 1), tail[1], 0, CUT - H)
            interleave("V", half(p2, 1), xraw[c - 2], 0, B)
            kq[c - 2], h = quant2(kh, "kh", 3, E5)
            kh = pair()
            for b in range(2):
                flip_four_copy(half(kh, 0), xts, b)
            if c == 2:
                interleave("S", half(p0, 0), first[c + 1][0], CUT, B)
                interleave("S", half(p0, 1), first[c + 1][1], MID, B)
            else:
                interleave("S", quarter(p0, 1), tail[1], CUT - H, H)
                interleave("S", quarter(p0, 2), tail[2], MID - H, H)
            o = [dx_mul(h, b, "w" + str(b), False) for b in range(2)]
            if c == 2:
                p1 = pair()
                interleave("V", half(p0, 1), first[c + 1][1], 0, MID)
                load_chunk(c + 2)
            a4, xq[c - 2] = quant2(p2, "ax", 2, E4)
            dh_four(4, a4)
            if c > 2:
                interleave("V", quarter(p0, 3), tail[3], 0, H)
                interleave("V", quarter(p0, 2), tail[2], 0, MID - H)
            for b in range(2):
                dx_store(c - 1, b, o[b])
            late = [dx_mul(h, b + 2, "w" + str(b), False) for b in range(2)]
            dw_mul(0, c - 2)
            dw_mul(1, c - 2)

        c = NB - 1
        wide = {}

        def wide_pass(u, b, a, g, start, stop):
            if start:
                wide[u, b] = bank("dh" + str(2 * u + b))
            for t in range(2):
                mm(wide[u, b][:, H * t : H * (t + 1)], gq[g], 2 * b + t, E5, a, E4, start and t == 0, stop and t == 1)

        d = new([P, 4 * B], BF16, "d", 3)

        def evict_wide(u, b, eng):
            copy(
                eng,
                d[:].rearrange("p (t v m e) -> p t v m e", t=4, v=2, e=2)[:, 2 * b : 2 * b + 2, :, 64 * u : 64 * (u + 1), :],
                wide[u, b][:].rearrange("p (t m v e) -> p t v m e", t=2, v=2, e=2),
            )

        def inter_half(dst, u):
            nc.vector.tensor_copy(
                out=dst.rearrange("p (e m v t) -> p m v t e", e=2, v=2, t=4),
                in_=d[:].rearrange("p (t v m e) -> p m v t e", t=4, v=2, e=2)[:, 64 * u : 64 * (u + 1)],
            )

        def dx_last(u, e, o, eng):
            t = out_half(e)
            copy(eng, t, o[:])
            lo = B * c + H * u
            nc.sync.dma_start(out=out_0[lo : lo + H, :].rearrange("(p e) w -> p e w", e=2)[:, e, :], in_=t)

        def dw_sum(a, k, tag=None, stop=False):
            if tag:
                acc[a] = bank(tag)
            mm(acc[a], xq[k], a, E4, kq[k], E5, tag is not None, stop)

        evict_four(half(kh, 1))
        p1, p2 = pair(), pair()
        interleave("V", quarter(p1, 0), tail[0], H, B, H)
        pa = part(codes("two", 2, 2), 0, 2 * B)
        quant(pa, p0[:], E4)
        for b in range(2):
            for g in range(4):
                wide_pass(0, b, part(pa, H * g, H * (g + 1)), g, g == 0, False)
        for b in range(2):
            dx_store(c - 2, b + 2, late[b])
        interleave("V", half(p2, 0), last[c], 0, B)
        interleave("V", quarter(p1, 1), tail[1], H, B, H)
        interleave("S", quarter(p1, 3), tail[3], H, B, H)
        a4 = quant1(half(p2, 0), "one", 4, E4)
        for b in range(2):
            wide_pass(0, b, part(a4, 0, H), NB - 1, False, True)
        xts3 = flip_four(half(kh, 1))
        kq[c - 2], h = quant2(kh, "kh", 3, E5)
        pb = part(codes("two", 2, 2), 0, 2 * B)
        quant(part(pb, 0, B), half(p1, 0), E4)
        for b in range(2):
            wide_pass(1, b, part(a4, H, B), NB - 1, True, False)
        for g in range(2):
            for b in range(2):
                wide_pass(1, b, part(pb, H * g, H * (g + 1)), g, False, False)
        for b in range(2):
            evict_wide(0, b, "S")
        o = [dx_mul(h, b, "dh" + str(b), False) for b in range(2)]
        hi, xx, kk = pair(), pair(), pair()
        interleave("V", quarter(p1, 2), tail[2], H, B, H)
        interleave("V", half(p2, 1), xraw[c - 2], 0, H)
        quant(part(pb, B, 2 * B), half(p1, 1), E4)
        for b in range(2):
            for g in range(2, 4):
                wide_pass(1, b, part(pb, H * g, H * (g + 1)), g, False, g == 3)
        for u in range(2):
            flip_four_copy(half(kk, 0), xts3, u)
        for b in range(2):
            dx_store(c - 1, b, o[b])
        o = [dx_mul(h, b + 2, "w" + str(b), False) for b in range(2)]
        hq = part(codes("one", 4, 1), 0, B)
        inter_half(quarter(hi, 0), 0)
        interleave("V", half(p2, 1), xraw[c - 2], H, B)
        quant(part(hq, 0, H), quarter(hi, 0), E5)
        xq[c - 2] = quant1(half(p2, 1), "x2", 1, E4)
        dw_sum(0, c - 2)
        dw_sum(1, c - 2)
        interleave("V", half(xx, 0), xraw[c - 1], 0, H)
        evict_wide(1, 1, "V")
        evict_wide(1, 0, "S")
        for b in range(2):
            dx_store(c - 1, b + 2, o[b])
        dw_sum(2, 0, "dh0")
        oa = [dx_mul(hq, 0, "w0", False)]
        dw_sum(2, 1)
        oa.append(dx_mul(hq, 1, "w1", False))
        xts = flip(d, ["dh2", "dh3"])
        for e in range(2):
            dx_last(0, e, oa[e], "S")
        kq[c - 1] = quant1(half(kk, 0), "one", 4, E5)
        inter_half(quarter(hi, 1), 1)
        interleave("V", half(xx, 0), xraw[c - 1], H, B)
        quant(part(hq, H, B), quarter(hi, 1), E5)
        dw_sum(2, 2)
        ob = [dx_mul(hq, 2 + e, "w" + str(e), False) for e in range(2)]
        for k in range(3):
            dw_sum(3, k, "dh1" if k == 0 else None)
        for b in range(2):
            flip_copy(half(kk, 1), xts, b, "S")
        xl = half(xx, 1)
        interleave("V", xl, xraw[c], 0, XV)
        xq[c - 1] = quant1(half(xx, 0), "one", 4, E4)
        dx_last(1, 0, ob[0], "S")
        interleave("S", xl, xraw[c], XV, B)
        kq[c] = quant1(half(kk, 1), "kl", 1, E5)
        xq[c] = part(codes("xl", 1, 1), 0, B)
        quant(part(xq[c], 0, H), quarter(xl, 0), E4)
        for a in range(2):
            dw_sum(a, c - 1)
        for a in range(2):
            dw_sum(a, c, stop=True)
        dx_last(1, 1, ob[1], "V")
        quant(part(xq[c], H, B), quarter(xl, 1), E4)
        for a in range(2, 4):
            dw_sum(a, c - 1)
        for a in range(2, 4):
            dw_sum(a, c, stop=True)
        for a in range(4):
            dw_store(a, "SVSV"[a])
